import numpy as np
import ml_dtypes


def mxq(x, axis, fmt="e4m3"):
    dtype, down = {"e4m3": (ml_dtypes.float8_e4m3fn, 7), "e5m2": (ml_dtypes.float8_e5m2, 14)}[fmt]
    v = np.moveaxis(np.asarray(x, np.float32).astype(ml_dtypes.bfloat16).astype(np.float64), axis, -1)
    blocks = v.reshape(v.shape[:-1] + (-1, 32))
    amax = np.abs(blocks).max(-1, keepdims=True)
    byte = np.maximum(np.where(amax > 0, np.frexp(amax)[1] - 1 + 127, 0) - down, 1)
    scale = np.exp2(byte - 127.0)
    codes = (blocks / scale).astype(np.float32).astype(dtype).astype(np.float64)
    return np.moveaxis((codes * scale).reshape(v.shape), -1, axis)


WIDE = False


def mx_kscale(k):
    if not WIDE:
        return np.ones(k)
    levels = np.array([10, -10, 5, -5, 0])
    a = np.random.permutation(np.resize(levels, k // 512 * 4)).reshape(k // 512, 4)
    idx = np.arange(k)
    return np.exp2(a[idx // 512, idx % 128 // 32])


BF16 = ml_dtypes.bfloat16


def bf(x):
    return np.asarray(x, np.float32).astype(BF16)


def f64(x):
    return np.asarray(x).astype(np.float64)


B, L, D, DK, DV = 1, 1024, 512, 256, 512


def skew(qe):
    b, l, m = qe.shape
    cat = np.concatenate([np.zeros((b, l, 1)), qe], axis=2)
    return cat.reshape(b, m + 1, l)[:, 1:, :]


def setup_inputs():
    s = mx_kscale(D)
    return {"q": bf(np.random.standard_normal((B, L, DK)) * 1.5),
            "k": bf(np.random.standard_normal((B, L, DK)) * 1.2),
            "inputV": bf(np.random.standard_normal((B, L, D)) * s),
            "Wv": bf(np.random.standard_normal((D, DV)) / np.sqrt(D) / s[:, None]),
            "E": bf(np.random.standard_normal((L, DK)))}


def reference(q, k, inputV, Wv, E):
    v = mxq(f64(inputV), 2, "e4m3") @ mxq(f64(Wv), 0, "e4m3")
    qe = f64(q) @ f64(E).T
    srel = skew(qe)
    qkt = f64(q) @ f64(k).transpose(0, 2, 1)
    sc = (qkt + srel) / np.sqrt(DK)
    e = np.exp(sc - sc.max(-1, keepdims=True))
    return (mxq(e, 2, "e4m3") @ mxq(v, 1, "e4m3")) / e.sum(-1, keepdims=True)

@@ -1,0 +1,284 @@
+from contextlib import ExitStack
+
+import concourse.mybir as mybir
+from concourse.masks import make_identity
+
+F32 = mybir.dt.float32
+BF16 = mybir.dt.bfloat16
+U32 = mybir.dt.uint32
+U8 = mybir.dt.uint8
+FP8X4 = mybir.dt.float8_e4m3fn_x4
+ACT = mybir.ActivationFunctionType
+ALU = mybir.AluOpType
+AXIS = mybir.AxisListType
+
+P = 128
+PACK = 4
+BANK = 512
+L, DK, D, DV = 1024, 256, 512, 512
+TILES = L // P
+KEY_PASSES = L // (P * PACK)
+SCALE = 1.0 / 16.0
+
+Z_COLS = L + P
+SLOTS = 3
+FIRST_SLOT = L * DV - SLOTS * P * Z_COLS
+
+FLOPS = 2 * L * (D * DV + 2 * L * DK + L * DV)
+
+
+def copy_out(nc, on_scalar, out, in_):
+    if on_scalar:
+        nc.scalar.copy(out=out, in_=in_)
+    else:
+        nc.vector.tensor_copy(out=out, in_=in_)
+
+
+def load_rows(nc, pool, src, label):
+    width = src.shape[1]
+    raw = pool.tile([P, TILES * width], BF16, name="%s_raw" % label)
+    nc.sync.dma_start(
+        out=raw[:].rearrange("p (t d) -> p t d", t=TILES),
+        in_=src.rearrange("(t p) d -> p t d", p=P),
+    )
+    return raw
+
+
+def transpose_pairs(nc, psum, ident_f32, raw, dst_words, on_scalar):
+    raw_words = raw[:].bitcast(F32)
+    for half in range(L // BANK):
+        bank = psum.tile([P, BANK], F32, name="pairs", tag="bank")
+        for s in range(BANK // P):
+            t = half * (BANK // P) + s
+            nc.tensor.transpose(bank[:, s * P : (s + 1) * P], raw_words[:, t * P : (t + 1) * P], ident_f32[:])
+        copy_out(nc, on_scalar, dst_words[:, half * BANK : (half + 1) * BANK], bank[:])
+
+
+def tile_relativeglobalattention_pa_kernel(tc, q, k, inputV, Wv, E, out):
+    nc = tc.nc
+    out_rows = out.flatten_outer_dims()
+    out_flat = out.rearrange("b l d -> (b l d)")
+
+    with ExitStack() as ctx:
+        const = ctx.enter_context(tc.tile_pool(name="const", bufs=1))
+        loads = ctx.enter_context(tc.tile_pool(name="loads", bufs=1))
+        keep = ctx.enter_context(tc.tile_pool(name="keep", bufs=1))
+        z_pool = ctx.enter_context(tc.tile_pool(name="z", bufs=4))
+        s_pool = ctx.enter_context(tc.tile_pool(name="s", bufs=TILES))
+        work = ctx.enter_context(tc.tile_pool(name="work", bufs=3))
+        small = ctx.enter_context(tc.tile_pool(name="small", bufs=4))
+        results = ctx.enter_context(tc.tile_pool(name="results", bufs=TILES))
+        psum = ctx.enter_context(tc.psum_pool(name="psum", bufs=8))
+
+        q_raw = load_rows(nc, loads, q.flatten_outer_dims(), "q")
+        e_raw = load_rows(nc, loads, E, "e")
+        k_raw = load_rows(nc, loads, k.flatten_outer_dims(), "k")
+        x_raw = load_rows(nc, loads, inputV.flatten_outer_dims(), "x")
+        w_raw = loads.tile([P, PACK * DV], BF16, name="w_raw")
+        nc.sync.dma_start(
+            out=w_raw[:].rearrange("p (u x) -> p u x", u=2),
+            in_=Wv.rearrange("(u p h) c -> p u (h c)", u=2, h=2),
+        )
+
+        ident_f32 = const.tile([P, P], F32, name="ident_f32")
+        make_identity(nc, ident_f32[:])
+        ident_bf16 = const.tile([P, P], BF16, name="ident_bf16")
+        make_identity(nc, ident_bf16[:])
+
+        qT = keep.tile([P, 2 * (L + 1)], BF16, name="qT")
+        eT = keep.tile([P, 2 * (L + 1)], BF16, name="eT")
+        kT = keep.tile([P, 2 * L], BF16, name="kT")
+        qT_words = qT[:].bitcast(F32)
+        eT_words = eT[:].bitcast(F32)
+        nc.vector.memset(qT_words[:, L : L + 1], 0.0)
+        nc.vector.memset(eT_words[:, 0:1], 0.0)
+        transpose_pairs(nc, psum, ident_f32, q_raw, qT_words[:, 0:L], True)
+        transpose_pairs(nc, psum, ident_f32, e_raw, eT_words[:, 1 : L + 1], False)
+        qT_pairs = qT[:].rearrange("p (c h) -> p c h", h=2)
+        eT_pairs = eT[:].rearrange("p (c h) -> p c h", h=2)
+        kT_pairs = kT[:].rearrange("p (c h) -> p c h", h=2)
+
+        srel = {}
+
+        def skewed_logits(i):
+            z = z_pool.tile([P, Z_COLS], F32, name="z")
+            first_part = (i + 1) * P
+            parts = (
+                (0, 1 + L - first_part, first_part, 0),
+                (1, 0, Z_COLS - first_part, first_part),
+            )
+            piece = 0
+            for next_query, e_first, width, z_first in parts:
+                queries = slice(i * P + next_query, (i + 1) * P + next_query)
+                for c in range(0, width, BANK):
+                    n = min(BANK, width - c)
+                    bank = psum.tile([P, BANK], F32, name="qe", tag="bank")
+                    for h in range(2):
+                        nc.tensor.matmul(
+                            out=bank[:, :n],
+                            lhsT=qT_pairs[:, queries, h],
+                            rhs=eT_pairs[:, e_first + c : e_first + c + n, h],
+                            start=(h == 0),
+                            stop=(h == 1),
+                        )
+                    copy_out(nc, (i + piece) % 2 == 0, z[:, z_first + c : z_first + c + n], bank[:, :n])
+                    piece += 1
+            base = FIRST_SLOT + (i % SLOTS) * P * Z_COLS
+            nc.sync.dma_start(
+                out=out_flat[base : base + P * Z_COLS].rearrange("(p t) -> p t", t=Z_COLS),
+                in_=z[:],
+            )
+            window = s_pool.tile([P, L], F32, name="window")
+            nc.gpsimd.dma_start(
+                out=window[:],
+                in_=out_flat[base + P - 1 : base + P - 1 + P * (Z_COLS - 1)].rearrange(
+                    "(p t) -> p t", t=Z_COLS - 1
+                )[:, 0:L],
+            )
+            srel[i] = window
+
+        for i in range(SLOTS):
+            skewed_logits(i)
+
+        transpose_pairs(nc, psum, ident_f32, k_raw, kT[:].bitcast(F32), True)
+
+        x_grouped = keep.tile([P, PACK * L], BF16, name="x_grouped", align_bytes=64)
+        x_codes = keep.tile([P, L], U32, name="x_codes", align_bytes=64)
+        x_scales = keep.tile([P, L], U8, name="x_scales", align_bytes=64)
+        x_words = x_raw[:].bitcast(F32)
+        x_grouped_words = x_grouped[:].bitcast(F32).rearrange("p (r u) -> p r u", u=2)
+        keys_per_bank = BANK // 2
+        for b in range(L // keys_per_bank):
+            bank = psum.tile([P, BANK], F32, name="xT", tag="bank")
+            for s in range(keys_per_bank // P):
+                t = b * (keys_per_bank // P) + s
+                for u in range(2):
+                    nc.tensor.transpose(
+                        bank[:, u * keys_per_bank + s * P : u * keys_per_bank + (s + 1) * P],
+                        x_words[:, (2 * t + u) * P : (2 * t + u + 1) * P],
+                        ident_f32[:],
+                    )
+            copy_out(
+                nc,
+                b % 2 == 0,
+                x_grouped_words[:, b * keys_per_bank : (b + 1) * keys_per_bank, :],
+                bank[:].rearrange("p (u r) -> p r u", u=2),
+            )
+
+        w_grouped = keep.tile([P, PACK * DV], BF16, name="w_grouped", align_bytes=64)
+        w_codes = keep.tile([P, DV], U32, name="w_codes", align_bytes=64)
+        w_scales = keep.tile([P, DV], U8, name="w_scales", align_bytes=64)
+        nc.vector.tensor_copy(
+            out=w_grouped[:].rearrange("p (c t) -> p c t", t=PACK),
+            in_=w_raw[:].rearrange("p (t c) -> p c t", t=PACK),
+        )
+        nc.vector.quantize_mx(out=w_codes[:].bitcast(FP8X4), scales=w_scales[:], in_=w_grouped[:])
+        nc.vector.quantize_mx(out=x_codes[:].bitcast(FP8X4), scales=x_scales[:], in_=x_grouped[:])
+
+        v_grouped = keep.tile([P, KEY_PASSES * PACK * DV], BF16, name="v_grouped", align_bytes=64)
+        v_codes = keep.tile([P, KEY_PASSES * DV], U32, name="v_codes", align_bytes=64)
+        v_scales = keep.tile([P, KEY_PASSES * DV], U8, name="v_scales", align_bytes=64)
+        for g in range(KEY_PASSES):
+            for c in range(DV // P):
+                bank = psum.tile([P, BANK], F32, name="v", tag="bank")
+                for j in range(PACK):
+                    keys = slice((PACK * g + j) * P, (PACK * g + j + 1) * P)
+                    nc.tensor.matmul_mx(
+                        out=bank[:, j * P : (j + 1) * P],
+                        lhsT=x_codes[:, keys].bitcast(FP8X4),
+                        lhsT_scale=x_scales[:, keys],
+                        rhs=w_codes[:, c * P : (c + 1) * P].bitcast(FP8X4),
+                        rhs_scale=w_scales[:, c * P : (c + 1) * P],
+                        start=True,
+                        stop=True,
+                    )
+                first = (g * DV + c * P) * PACK
+                copy_out(
+                    nc,
+                    c % 2 == 0,
+                    v_grouped[:, first : first + P * PACK].rearrange("p (w j) -> p w j", j=PACK),
+                    bank[:].rearrange("p (j w) -> p w j", j=PACK),
+                )
+            nc.vector.quantize_mx(
+                out=v_codes[:, g * DV : (g + 1) * DV].bitcast(FP8X4),
+                scales=v_scales[:, g * DV : (g + 1) * DV],
+                in_=v_grouped[:, g * DV * PACK : (g + 1) * DV * PACK],
+            )
+
+        e_rows = {}
+        row_sums = {}
+        finished = {}
+
+        def scores_and_exp(i):
+            s = srel[i]
+            for half in range(L // BANK):
+                cols = slice(half * BANK, (half + 1) * BANK)
+                bank = psum.tile([P, BANK], F32, name="qk", tag="bank")
+                for h in range(2):
+                    nc.tensor.matmul(
+                        out=bank[:],
+                        lhsT=qT_pairs[:, i * P : (i + 1) * P, h],
+                        rhs=kT_pairs[:, cols, h],
+                        start=(h == 0),
+                        stop=(h == 1),
+                    )
+                nc.vector.tensor_tensor(out=s[:, cols], in0=bank[:], in1=s[:, cols], op=ALU.add)
+            row_max = small.tile([P, 1], F32, name="row_max")
+            nc.vector.reduce_max(out=row_max[:], in_=s[:], axis=AXIS.X)
+            shift = small.tile([P, 1], F32, name="shift")
+            nc.vector.tensor_scalar_mul(out=shift[:], in0=row_max[:], scalar1=-SCALE)
+            e_bf16 = work.tile([P, L], BF16, name="e_bf16")
+            row_sum = small.tile([P, 1], F32, name="row_sum")
+            nc.scalar.activation(
+                out=e_bf16[:], in_=s[:], func=ACT.Exp, bias=shift[:], scale=SCALE, accum_out=row_sum[:]
+            )
+            e_rows[i] = e_bf16
+            row_sums[i] = row_sum
+
+        def weighted_values(i):
+            keys_first = psum.tile([P, L], BF16, name="keys_first", tag="bank")
+            for t in range(TILES):
+                nc.tensor.transpose(
+                    keys_first[:, t * P : (t + 1) * P], e_rows[i][:, t * P : (t + 1) * P], ident_bf16[:]
+                )
+            e_grouped = work.tile([P, L], BF16, name="e_grouped", align_bytes=64)
+            nc.scalar.copy(
+                out=e_grouped[:].rearrange("p (g w j) -> p g w j", g=KEY_PASSES, j=PACK),
+                in_=keys_first[:].rearrange("p (g j w) -> p g w j", g=KEY_PASSES, j=PACK),
+            )
+            e_codes = work.tile([P, KEY_PASSES * P], U32, name="e_codes", align_bytes=64)
+            e_scales = work.tile([P, KEY_PASSES * P], U8, name="e_scales", align_bytes=64)
+            nc.vector.quantize_mx(out=e_codes[:].bitcast(FP8X4), scales=e_scales[:], in_=e_grouped[:])
+            acc = psum.tile([P, DV], F32, name="acc", tag="bank")
+            for g in range(KEY_PASSES):
+                nc.tensor.matmul_mx(
+                    out=acc[:],
+                    lhsT=e_codes[:, g * P : (g + 1) * P].bitcast(FP8X4),
+                    lhsT_scale=e_scales[:, g * P : (g + 1) * P],
+                    rhs=v_codes[:, g * DV : (g + 1) * DV].bitcast(FP8X4),
+                    rhs_scale=v_scales[:, g * DV : (g + 1) * DV],
+                    start=(g == 0),
+                    stop=(g == KEY_PASSES - 1),
+                )
+            inverse = small.tile([P, 1], F32, name="inverse")
+            nc.vector.reciprocal(out=inverse[:], in_=row_sums[i][:])
+            result = results.tile([P, DV], F32, name="result")
+            nc.scalar.activation(out=result[:], in_=acc[:], func=ACT.Copy, scale=inverse[:])
+            finished[i] = result
+
+        def store_result(i):
+            nc.sync.dma_start(out=out_rows[i * P : (i + 1) * P, :], in_=finished[i][:])
+
+        last_scratch_step = TILES - SLOTS - 1
+        for i in range(TILES + 1):
+            if i + SLOTS < TILES:
+                skewed_logits(i + SLOTS)
+            if i < TILES:
+                scores_and_exp(i)
+            if i >= 1:
+                weighted_values(i - 1)
+            if i == last_scratch_step:
+                for t in range(i):
+                    store_result(t)
+            if i > last_scratch_step:
+                store_result(i - 1)

@@ -47,11 +47,11 @@ def load_rows(nc, pool, src, label):
 def transpose_pairs(nc, psum, ident_f32, raw, dst_words, on_scalar):
     raw_words = raw[:].bitcast(F32)
     for half in range(L // BANK):
-        bank = psum.tile([P, BANK], F32, name="pairs", tag="bank")
+        bank = psum.tile([P, BANK], F32, name="bank")
         for s in range(BANK // P):
             t = half * (BANK // P) + s
             nc.tensor.transpose(bank[:, s * P : (s + 1) * P], raw_words[:, t * P : (t + 1) * P], ident_f32[:])
-        copy_out(nc, on_scalar, dst_words[:, half * BANK : (half + 1) * BANK], bank[:])
+        copy_out(nc, on_scalar[half], dst_words[:, half * BANK : (half + 1) * BANK], bank[:])
 
 
 def tile_relativeglobalattention_pa_kernel(tc, q, k, inputV, Wv, E, out):
@@ -60,15 +60,15 @@ def tile_relativeglobalattention_pa_kernel(tc, q, k, inputV, Wv, E, out):
     out_flat = out.rearrange("b l d -> (b l d)")
 
     with ExitStack() as ctx:
+        ctx.enter_context(tc.manual_schedule())
         const = ctx.enter_context(tc.tile_pool(name="const", bufs=1))
         loads = ctx.enter_context(tc.tile_pool(name="loads", bufs=1))
         keep = ctx.enter_context(tc.tile_pool(name="keep", bufs=1))
         z_pool = ctx.enter_context(tc.tile_pool(name="z", bufs=4))
         s_pool = ctx.enter_context(tc.tile_pool(name="s", bufs=TILES))
         work = ctx.enter_context(tc.tile_pool(name="work", bufs=3))
-        small = ctx.enter_context(tc.tile_pool(name="small", bufs=4))
-        results = ctx.enter_context(tc.tile_pool(name="results", bufs=TILES))
-        psum = ctx.enter_context(tc.psum_pool(name="psum", bufs=8))
+        small = ctx.enter_context(tc.tile_pool(name="small", bufs=5))
+        results = ctx.enter_context(tc.tile_pool(name="results", bufs=4))
 
         q_raw = load_rows(nc, loads, q.flatten_outer_dims(), "q")
         e_raw = load_rows(nc, loads, E, "e")
@@ -85,22 +85,28 @@ def tile_relativeglobalattention_pa_kernel(tc, q, k, inputV, Wv, E, out):
         ident_bf16 = const.tile([P, P], BF16, name="ident_bf16")
         make_identity(nc, ident_bf16[:])
 
+        zero = const.tile([P, 1], F32, name="zero")
+        one = const.tile([P, 1], F32, name="one")
+        nc.vector.memset(zero[:], 0.0)
+        nc.scalar.activation(out=one[:], in_=zero[:], func=ACT.Exp)
+
         qT = keep.tile([P, 2 * (L + 1)], BF16, name="qT")
         eT = keep.tile([P, 2 * (L + 1)], BF16, name="eT")
         kT = keep.tile([P, 2 * L], BF16, name="kT")
         qT_words = qT[:].bitcast(F32)
         eT_words = eT[:].bitcast(F32)
-        nc.vector.memset(qT_words[:, L : L + 1], 0.0)
-        nc.vector.memset(eT_words[:, 0:1], 0.0)
-        transpose_pairs(nc, psum, ident_f32, q_raw, qT_words[:, 0:L], True)
-        transpose_pairs(nc, psum, ident_f32, e_raw, eT_words[:, 1 : L + 1], False)
         qT_pairs = qT[:].rearrange("p (c h) -> p c h", h=2)
         eT_pairs = eT[:].rearrange("p (c h) -> p c h", h=2)
         kT_pairs = kT[:].rearrange("p (c h) -> p c h", h=2)
 
         srel = {}
+        shifts = {}
+        e_rows = {}
+        row_sums = {}
+        e_keys_first = {}
+        e_quantised = {}
 
-        def skewed_logits(i):
+        def store_z(psum, i):
             z = z_pool.tile([P, Z_COLS], F32, name="z")
             first_part = (i + 1) * P
             parts = (
@@ -112,7 +118,7 @@ def tile_relativeglobalattention_pa_kernel(tc, q, k, inputV, Wv, E, out):
                 queries = slice(i * P + next_query, (i + 1) * P + next_query)
                 for c in range(0, width, BANK):
                     n = min(BANK, width - c)
-                    bank = psum.tile([P, BANK], F32, name="qe", tag="bank")
+                    bank = psum.tile([P, BANK], F32, name="bank")
                     for h in range(2):
                         nc.tensor.matmul(
                             out=bank[:, :n],
@@ -128,8 +134,11 @@ def tile_relativeglobalattention_pa_kernel(tc, q, k, inputV, Wv, E, out):
                 out=out_flat[base : base + P * Z_COLS].rearrange("(p t) -> p t", t=Z_COLS),
                 in_=z[:],
             )
+
+        def read_windows(i):
+            base = FIRST_SLOT + (i % SLOTS) * P * Z_COLS
             window = s_pool.tile([P, L], F32, name="window")
-            nc.gpsimd.dma_start(
+            nc.sync.dma_start(
                 out=window[:],
                 in_=out_flat[base + P - 1 : base + P - 1 + P * (Z_COLS - 1)].rearrange(
                     "(p t) -> p t", t=Z_COLS - 1
@@ -137,83 +146,11 @@ def tile_relativeglobalattention_pa_kernel(tc, q, k, inputV, Wv, E, out):
             )
             srel[i] = window
 
-        for i in range(SLOTS):
-            skewed_logits(i)
-
-        transpose_pairs(nc, psum, ident_f32, k_raw, kT[:].bitcast(F32), True)
-
-        x_grouped = keep.tile([P, PACK * L], BF16, name="x_grouped", align_bytes=64)
-        x_codes = keep.tile([P, L], U32, name="x_codes", align_bytes=64)
-        x_scales = keep.tile([P, L], U8, name="x_scales", align_bytes=64)
-        x_words = x_raw[:].bitcast(F32)
-        x_grouped_words = x_grouped[:].bitcast(F32).rearrange("p (r u) -> p r u", u=2)
-        keys_per_bank = BANK // 2
-        for b in range(L // keys_per_bank):
-            bank = psum.tile([P, BANK], F32, name="xT", tag="bank")
-            for s in range(keys_per_bank // P):
-                t = b * (keys_per_bank // P) + s
-                for u in range(2):
-                    nc.tensor.transpose(
-                        bank[:, u * keys_per_bank + s * P : u * keys_per_bank + (s + 1) * P],
-                        x_words[:, (2 * t + u) * P : (2 * t + u + 1) * P],
-                        ident_f32[:],
-                    )
-            copy_out(
-                nc,
-                b % 2 == 0,
-                x_grouped_words[:, b * keys_per_bank : (b + 1) * keys_per_bank, :],
-                bank[:].rearrange("p (u r) -> p r u", u=2),
-            )
-
-        w_grouped = keep.tile([P, PACK * DV], BF16, name="w_grouped", align_bytes=64)
-        w_codes = keep.tile([P, DV], U32, name="w_codes", align_bytes=64)
-        w_scales = keep.tile([P, DV], U8, name="w_scales", align_bytes=64)
-        nc.vector.tensor_copy(
-            out=w_grouped[:].rearrange("p (c t) -> p c t", t=PACK),
-            in_=w_raw[:].rearrange("p (t c) -> p c t", t=PACK),
-        )
-        nc.vector.quantize_mx(out=w_codes[:].bitcast(FP8X4), scales=w_scales[:], in_=w_grouped[:])
-        nc.vector.quantize_mx(out=x_codes[:].bitcast(FP8X4), scales=x_scales[:], in_=x_grouped[:])
-
-        v_grouped = keep.tile([P, KEY_PASSES * PACK * DV], BF16, name="v_grouped", align_bytes=64)
-        v_codes = keep.tile([P, KEY_PASSES * DV], U32, name="v_codes", align_bytes=64)
-        v_scales = keep.tile([P, KEY_PASSES * DV], U8, name="v_scales", align_bytes=64)
-        for g in range(KEY_PASSES):
-            for c in range(DV // P):
-                bank = psum.tile([P, BANK], F32, name="v", tag="bank")
-                for j in range(PACK):
-                    keys = slice((PACK * g + j) * P, (PACK * g + j + 1) * P)
-                    nc.tensor.matmul_mx(
-                        out=bank[:, j * P : (j + 1) * P],
-                        lhsT=x_codes[:, keys].bitcast(FP8X4),
-                        lhsT_scale=x_scales[:, keys],
-                        rhs=w_codes[:, c * P : (c + 1) * P].bitcast(FP8X4),
-                        rhs_scale=w_scales[:, c * P : (c + 1) * P],
-                        start=True,
-                        stop=True,
-                    )
-                first = (g * DV + c * P) * PACK
-                copy_out(
-                    nc,
-                    c % 2 == 0,
-                    v_grouped[:, first : first + P * PACK].rearrange("p (w j) -> p w j", j=PACK),
-                    bank[:].rearrange("p (j w) -> p w j", j=PACK),
-                )
-            nc.vector.quantize_mx(
-                out=v_codes[:, g * DV : (g + 1) * DV].bitcast(FP8X4),
-                scales=v_scales[:, g * DV : (g + 1) * DV],
-                in_=v_grouped[:, g * DV * PACK : (g + 1) * DV * PACK],
-            )
-
-        e_rows = {}
-        row_sums = {}
-        finished = {}
-
-        def scores_and_exp(i):
+        def scores(psum, i):
             s = srel[i]
             for half in range(L // BANK):
                 cols = slice(half * BANK, (half + 1) * BANK)
-                bank = psum.tile([P, BANK], F32, name="qk", tag="bank")
+                bank = psum.tile([P, BANK], F32, name="bank")
                 for h in range(2):
                     nc.tensor.matmul(
                         out=bank[:],
@@ -227,29 +164,37 @@ def tile_relativeglobalattention_pa_kernel(tc, q, k, inputV, Wv, E, out):
             nc.vector.reduce_max(out=row_max[:], in_=s[:], axis=AXIS.X)
             shift = small.tile([P, 1], F32, name="shift")
             nc.vector.tensor_scalar_mul(out=shift[:], in0=row_max[:], scalar1=-SCALE)
+            shifts[i] = shift
+
+        def exponentials(i):
             e_bf16 = work.tile([P, L], BF16, name="e_bf16")
             row_sum = small.tile([P, 1], F32, name="row_sum")
             nc.scalar.activation(
-                out=e_bf16[:], in_=s[:], func=ACT.Exp, bias=shift[:], scale=SCALE, accum_out=row_sum[:]
+                out=e_bf16[:], in_=srel[i][:], func=ACT.Exp, bias=shifts[i][:], scale=SCALE, accum_out=row_sum[:]
             )
             e_rows[i] = e_bf16
             row_sums[i] = row_sum
 
-        def weighted_values(i):
-            keys_first = psum.tile([P, L], BF16, name="keys_first", tag="bank")
+        def transpose_e(psum, i):
+            bank = psum.tile([P, L], BF16, name="bank")
             for t in range(TILES):
-                nc.tensor.transpose(
-                    keys_first[:, t * P : (t + 1) * P], e_rows[i][:, t * P : (t + 1) * P], ident_bf16[:]
-                )
+                nc.tensor.transpose(bank[:, t * P : (t + 1) * P], e_rows[i][:, t * P : (t + 1) * P], ident_bf16[:])
+            e_keys_first[i] = bank
+
+        def quantise_e(i):
             e_grouped = work.tile([P, L], BF16, name="e_grouped", align_bytes=64)
             nc.scalar.copy(
                 out=e_grouped[:].rearrange("p (g w j) -> p g w j", g=KEY_PASSES, j=PACK),
-                in_=keys_first[:].rearrange("p (g j w) -> p g w j", g=KEY_PASSES, j=PACK),
+                in_=e_keys_first[i][:].rearrange("p (g j w) -> p g w j", g=KEY_PASSES, j=PACK),
             )
             e_codes = work.tile([P, KEY_PASSES * P], U32, name="e_codes", align_bytes=64)
             e_scales = work.tile([P, KEY_PASSES * P], U8, name="e_scales", align_bytes=64)
             nc.vector.quantize_mx(out=e_codes[:].bitcast(FP8X4), scales=e_scales[:], in_=e_grouped[:])
-            acc = psum.tile([P, DV], F32, name="acc", tag="bank")
+            e_quantised[i] = (e_codes, e_scales)
+
+        def weighted_values(psum, i):
+            e_codes, e_scales = e_quantised[i]
+            acc = psum.tile([P, DV], F32, name="bank")
             for g in range(KEY_PASSES):
                 nc.tensor.matmul_mx(
                     out=acc[:],
@@ -264,21 +209,102 @@ def tile_relativeglobalattention_pa_kernel(tc, q, k, inputV, Wv, E, out):
             nc.vector.reciprocal(out=inverse[:], in_=row_sums[i][:])
             result = results.tile([P, DV], F32, name="result")
             nc.scalar.activation(out=result[:], in_=acc[:], func=ACT.Copy, scale=inverse[:])
-            finished[i] = result
+            nc.sync.dma_start(out=out_rows[i * P : (i + 1) * P, :], in_=result[:])
 
-        def store_result(i):
-            nc.sync.dma_start(out=out_rows[i * P : (i + 1) * P, :], in_=finished[i][:])
+        with tc.psum_pool(name="psum_head", bufs=8) as psum:
+            nc.vector.memset(qT_words[:, L : L + 1], 0.0)
+            nc.vector.memset(eT_words[:, 0:1], 0.0)
+            transpose_pairs(nc, psum, ident_f32, q_raw, qT_words[:, 0:L], (True, True))
+            transpose_pairs(nc, psum, ident_f32, e_raw, eT_words[:, 1 : L + 1], (False, False))
 
-        last_scratch_step = TILES - SLOTS - 1
-        for i in range(TILES + 1):
-            if i + SLOTS < TILES:
-                skewed_logits(i + SLOTS)
-            if i < TILES:
-                scores_and_exp(i)
-            if i >= 1:
-                weighted_values(i - 1)
-            if i == last_scratch_step:
-                for t in range(i):
-                    store_result(t)
-            if i > last_scratch_step:
-                store_result(i - 1)
+            for i in range(SLOTS):
+                store_z(psum, i)
+            for i in range(SLOTS):
+                read_windows(i)
+
+            transpose_pairs(nc, psum, ident_f32, k_raw, kT[:].bitcast(F32), (True, False))
+
+            w_grouped = keep.tile([P, PACK * DV], BF16, name="w_grouped", align_bytes=64)
+            w_codes = keep.tile([P, DV], U32, name="w_codes", align_bytes=64)
+            w_scales = keep.tile([P, DV], U8, name="w_scales", align_bytes=64)
+            nc.vector.tensor_copy(
+                out=w_grouped[:].rearrange("p (c t) -> p c t", t=PACK),
+                in_=w_raw[:].rearrange("p (t c) -> p c t", t=PACK),
+            )
+
+            x_grouped = keep.tile([P, PACK * L], BF16, name="x_grouped", align_bytes=64)
+            x_codes = keep.tile([P, L], U32, name="x_codes", align_bytes=64)
+            x_scales = keep.tile([P, L], U8, name="x_scales", align_bytes=64)
+            x_words = x_raw[:].bitcast(F32)
+            x_grouped_words = x_grouped[:].bitcast(F32).rearrange("p (r u) -> p r u", u=2)
+            keys_per_bank = BANK // 2
+            for b in range(L // keys_per_bank):
+                bank = psum.tile([P, BANK], F32, name="bank")
+                for s in range(keys_per_bank // P):
+                    t = b * (keys_per_bank // P) + s
+                    for u in range(2):
+                        nc.tensor.transpose(
+                            bank[:, u * keys_per_bank + s * P : u * keys_per_bank + (s + 1) * P],
+                            x_words[:, (2 * t + u) * P : (2 * t + u + 1) * P],
+                            ident_f32[:],
+                        )
+                copy_out(
+                    nc,
+                    b % 2 == 0,
+                    x_grouped_words[:, b * keys_per_bank : (b + 1) * keys_per_bank, :],
+                    bank[:].rearrange("p (u r) -> p r u", u=2),
+                )
+            nc.vector.quantize_mx(out=w_codes[:].bitcast(FP8X4), scales=w_scales[:], in_=w_grouped[:])
+            nc.vector.quantize_mx(out=x_codes[:].bitcast(FP8X4), scales=x_scales[:], in_=x_grouped[:])
+
+            v_grouped = keep.tile([P, KEY_PASSES * PACK * DV], BF16, name="v_grouped", align_bytes=64)
+            v_codes = keep.tile([P, KEY_PASSES * DV], U32, name="v_codes", align_bytes=64)
+            v_scales = keep.tile([P, KEY_PASSES * DV], U8, name="v_scales", align_bytes=64)
+            for g in range(KEY_PASSES):
+                for c in range(DV // P):
+                    bank = psum.tile([P, BANK], F32, name="bank")
+                    for j in range(PACK):
+                        keys = slice((PACK * g + j) * P, (PACK * g + j + 1) * P)
+                        nc.tensor.matmul_mx(
+                            out=bank[:, j * P : (j + 1) * P],
+                            lhsT=x_codes[:, keys].bitcast(FP8X4),
+                            lhsT_scale=x_scales[:, keys],
+                            rhs=w_codes[:, c * P : (c + 1) * P].bitcast(FP8X4),
+                            rhs_scale=w_scales[:, c * P : (c + 1) * P],
+                            start=True,
+                            stop=True,
+                        )
+                    first = (g * DV + c * P) * PACK
+                    copy_out(
+                        nc,
+                        c % 2 == 0,
+                        v_grouped[:, first : first + P * PACK].rearrange("p (w j) -> p w j", j=PACK),
+                        bank[:].rearrange("p (j w) -> p w j", j=PACK),
+                    )
+            for g in range(KEY_PASSES):
+                nc.vector.quantize_mx(
+                    out=v_codes[:, g * DV : (g + 1) * DV].bitcast(FP8X4),
+                    scales=v_scales[:, g * DV : (g + 1) * DV],
+                    in_=v_grouped[:, g * DV * PACK : (g + 1) * DV * PACK],
+                )
+
+        assert P * DV <= FIRST_SLOT
+        with ExitStack() as banks:
+            psum_z = banks.enter_context(tc.psum_pool(name="psum_z", bufs=3))
+            psum_s = banks.enter_context(tc.psum_pool(name="psum_s", bufs=2))
+            psum_e = banks.enter_context(tc.psum_pool(name="psum_e", bufs=2))
+            psum_o = banks.enter_context(tc.psum_pool(name="psum_o", bufs=1))
+            for n in range(TILES + 3):
+                if n + SLOTS < TILES:
+                    store_z(psum_z, n + SLOTS)
+                    read_windows(n + SLOTS)
+                if n < TILES:
+                    scores(psum_s, n)
+                if 0 <= n - 1 < TILES:
+                    exponentials(n - 1)
+                if 0 <= n - 3 < TILES:
+                    weighted_values(psum_o, n - 3)
+                if 0 <= n - 1 < TILES:
+                    transpose_e(psum_e, n - 1)
+                if 0 <= n - 2 < TILES:
+                    quantise_e(n - 2)

@@ -64,7 +64,7 @@ def tile_relativeglobalattention_pa_kernel(tc, q, k, inputV, Wv, E, out):
         const = ctx.enter_context(tc.tile_pool(name="const", bufs=1))
         loads = ctx.enter_context(tc.tile_pool(name="loads", bufs=1))
         keep = ctx.enter_context(tc.tile_pool(name="keep", bufs=1))
-        z_pool = ctx.enter_context(tc.tile_pool(name="z", bufs=4))
+        z_pool = ctx.enter_context(tc.tile_pool(name="z", bufs=5))
         s_pool = ctx.enter_context(tc.tile_pool(name="s", bufs=TILES))
         work = ctx.enter_context(tc.tile_pool(name="work", bufs=3))
         small = ctx.enter_context(tc.tile_pool(name="small", bufs=5))
@@ -72,13 +72,13 @@ def tile_relativeglobalattention_pa_kernel(tc, q, k, inputV, Wv, E, out):
 
         q_raw = load_rows(nc, loads, q.flatten_outer_dims(), "q")
         e_raw = load_rows(nc, loads, E, "e")
-        k_raw = load_rows(nc, loads, k.flatten_outer_dims(), "k")
         x_raw = load_rows(nc, loads, inputV.flatten_outer_dims(), "x")
         w_raw = loads.tile([P, PACK * DV], BF16, name="w_raw")
         nc.sync.dma_start(
             out=w_raw[:].rearrange("p (u x) -> p u x", u=2),
             in_=Wv.rearrange("(u p h) c -> p u (h c)", u=2, h=2),
         )
+        k_raw = load_rows(nc, loads, k.flatten_outer_dims(), "k")
 
         ident_f32 = const.tile([P, P], F32, name="ident_f32")
         make_identity(nc, ident_f32[:])
@@ -105,6 +105,8 @@ def tile_relativeglobalattention_pa_kernel(tc, q, k, inputV, Wv, E, out):
         row_sums = {}
         e_keys_first = {}
         e_quantised = {}
+        sums = {}
+        inverses = {}
 
         def store_z(psum, i):
             z = z_pool.tile([P, Z_COLS], F32, name="z")
@@ -127,7 +129,7 @@ def tile_relativeglobalattention_pa_kernel(tc, q, k, inputV, Wv, E, out):
                             start=(h == 0),
                             stop=(h == 1),
                         )
-                    copy_out(nc, (i + piece) % 2 == 0, z[:, z_first + c : z_first + c + n], bank[:, :n])
+                    copy_out(nc, piece != 1, z[:, z_first + c : z_first + c + n], bank[:, :n])
                     piece += 1
             base = FIRST_SLOT + (i % SLOTS) * P * Z_COLS
             nc.sync.dma_start(
@@ -182,6 +184,9 @@ def tile_relativeglobalattention_pa_kernel(tc, q, k, inputV, Wv, E, out):
             e_keys_first[i] = bank
 
         def quantise_e(i):
+            inverse = small.tile([P, 1], F32, name="inverse")
+            nc.vector.reciprocal(out=inverse[:], in_=row_sums[i][:])
+            inverses[i] = inverse
             e_grouped = work.tile([P, L], BF16, name="e_grouped", align_bytes=64)
             nc.scalar.copy(
                 out=e_grouped[:].rearrange("p (g w j) -> p g w j", g=KEY_PASSES, j=PACK),
@@ -192,7 +197,7 @@ def tile_relativeglobalattention_pa_kernel(tc, q, k, inputV, Wv, E, out):
             nc.vector.quantize_mx(out=e_codes[:].bitcast(FP8X4), scales=e_scales[:], in_=e_grouped[:])
             e_quantised[i] = (e_codes, e_scales)
 
-        def weighted_values(psum, i):
+        def multiply_e_v(psum, i):
             e_codes, e_scales = e_quantised[i]
             acc = psum.tile([P, DV], F32, name="bank")
             for g in range(KEY_PASSES):
@@ -205,10 +210,14 @@ def tile_relativeglobalattention_pa_kernel(tc, q, k, inputV, Wv, E, out):
                     start=(g == 0),
                     stop=(g == KEY_PASSES - 1),
                 )
-            inverse = small.tile([P, 1], F32, name="inverse")
-            nc.vector.reciprocal(out=inverse[:], in_=row_sums[i][:])
+            sums[i] = acc
+
+        def normalise_and_store(i):
             result = results.tile([P, DV], F32, name="result")
-            nc.scalar.activation(out=result[:], in_=acc[:], func=ACT.Copy, scale=inverse[:])
+            if i % 2 == 0:
+                nc.scalar.activation(out=result[:], in_=sums[i][:], func=ACT.Copy, scale=inverses[i][:])
+            else:
+                nc.vector.tensor_scalar_mul(out=result[:], in0=sums[i][:], scalar1=inverses[i][:])
             nc.sync.dma_start(out=out_rows[i * P : (i + 1) * P, :], in_=result[:])
 
         with tc.psum_pool(name="psum_head", bufs=8) as psum:
@@ -219,10 +228,8 @@ def tile_relativeglobalattention_pa_kernel(tc, q, k, inputV, Wv, E, out):
 
             for i in range(SLOTS):
                 store_z(psum, i)
-            for i in range(SLOTS):
+            for i in range(SLOTS - 1):
                 read_windows(i)
-
-            transpose_pairs(nc, psum, ident_f32, k_raw, kT[:].bitcast(F32), (True, False))
 
             w_grouped = keep.tile([P, PACK * DV], BF16, name="w_grouped", align_bytes=64)
             w_codes = keep.tile([P, DV], U32, name="w_codes", align_bytes=64)
@@ -238,6 +245,15 @@ def tile_relativeglobalattention_pa_kernel(tc, q, k, inputV, Wv, E, out):
             x_words = x_raw[:].bitcast(F32)
             x_grouped_words = x_grouped[:].bitcast(F32).rearrange("p (r u) -> p r u", u=2)
             keys_per_bank = BANK // 2
+
+            def quantise_x(b):
+                keys = slice(b * keys_per_bank, (b + 1) * keys_per_bank)
+                nc.vector.quantize_mx(
+                    out=x_codes[:, keys].bitcast(FP8X4),
+                    scales=x_scales[:, keys],
+                    in_=x_grouped[:, b * keys_per_bank * PACK : (b + 1) * keys_per_bank * PACK],
+                )
+
             for b in range(L // keys_per_bank):
                 bank = psum.tile([P, BANK], F32, name="bank")
                 for s in range(keys_per_bank // P):
@@ -254,13 +270,18 @@ def tile_relativeglobalattention_pa_kernel(tc, q, k, inputV, Wv, E, out):
                     x_grouped_words[:, b * keys_per_bank : (b + 1) * keys_per_bank, :],
                     bank[:].rearrange("p (u r) -> p r u", u=2),
                 )
-            nc.vector.quantize_mx(out=w_codes[:].bitcast(FP8X4), scales=w_scales[:], in_=w_grouped[:])
-            nc.vector.quantize_mx(out=x_codes[:].bitcast(FP8X4), scales=x_scales[:], in_=x_grouped[:])
+                if b == 0:
+                    nc.vector.quantize_mx(out=w_codes[:].bitcast(FP8X4), scales=w_scales[:], in_=w_grouped[:])
+                if b >= 1:
+                    quantise_x(b - 1)
+            quantise_x(L // keys_per_bank - 1)
+            transpose_pairs(nc, psum, ident_f32, k_raw, kT[:].bitcast(F32), (True, False))
 
             v_grouped = keep.tile([P, KEY_PASSES * PACK * DV], BF16, name="v_grouped", align_bytes=64)
             v_codes = keep.tile([P, KEY_PASSES * DV], U32, name="v_codes", align_bytes=64)
             v_scales = keep.tile([P, KEY_PASSES * DV], U8, name="v_scales", align_bytes=64)
-            for g in range(KEY_PASSES):
+
+            def project_values(psum, g):
                 for c in range(DV // P):
                     bank = psum.tile([P, BANK], F32, name="bank")
                     for j in range(PACK):
@@ -275,18 +296,21 @@ def tile_relativeglobalattention_pa_kernel(tc, q, k, inputV, Wv, E, out):
                             stop=True,
                         )
                     first = (g * DV + c * P) * PACK
-                    copy_out(
-                        nc,
-                        c % 2 == 0,
-                        v_grouped[:, first : first + P * PACK].rearrange("p (w j) -> p w j", j=PACK),
-                        bank[:].rearrange("p (j w) -> p w j", j=PACK),
+                    nc.scalar.copy(
+                        out=v_grouped[:, first : first + P * PACK].rearrange("p (w j) -> p w j", j=PACK),
+                        in_=bank[:].rearrange("p (j w) -> p w j", j=PACK),
                     )
-            for g in range(KEY_PASSES):
+
+            def quantise_values(g):
                 nc.vector.quantize_mx(
                     out=v_codes[:, g * DV : (g + 1) * DV].bitcast(FP8X4),
                     scales=v_scales[:, g * DV : (g + 1) * DV],
                     in_=v_grouped[:, g * DV * PACK : (g + 1) * DV * PACK],
                 )
+
+            store_z(psum, SLOTS)
+            read_windows(SLOTS - 1)
+            project_values(psum, 0)
 
         assert P * DV <= FIRST_SLOT
         with ExitStack() as banks:
@@ -295,16 +319,23 @@ def tile_relativeglobalattention_pa_kernel(tc, q, k, inputV, Wv, E, out):
             psum_e = banks.enter_context(tc.psum_pool(name="psum_e", bufs=2))
             psum_o = banks.enter_context(tc.psum_pool(name="psum_o", bufs=1))
             for n in range(TILES + 3):
-                if n + SLOTS < TILES:
-                    store_z(psum_z, n + SLOTS)
-                    read_windows(n + SLOTS)
-                if n < TILES:
-                    scores(psum_s, n)
                 if 0 <= n - 1 < TILES:
                     exponentials(n - 1)
+                if n < TILES:
+                    scores(psum_s, n)
+                if n < KEY_PASSES:
+                    quantise_values(n)
+                if n + SLOTS + 1 < TILES:
+                    store_z(psum_z, n + SLOTS + 1)
+                if n + SLOTS < TILES:
+                    read_windows(n + SLOTS)
                 if 0 <= n - 3 < TILES:
-                    weighted_values(psum_o, n - 3)
+                    multiply_e_v(psum_o, n - 3)
+                if n == 0:
+                    project_values(psum_e, 1)
                 if 0 <= n - 1 < TILES:
                     transpose_e(psum_e, n - 1)
                 if 0 <= n - 2 < TILES:
                     quantise_e(n - 2)
+                if 0 <= n - 3 < TILES:
+                    normalise_and_store(n - 3)

@@ -18,6 +18,7 @@ BANK = 512
 L, DK, D, DV = 1024, 256, 512, 512
 TILES = L // P
 KEY_PASSES = L // (P * PACK)
+X_KEYS = BANK // 2
 SCALE = 1.0 / 16.0
 
 Z_COLS = L + P
@@ -72,13 +73,13 @@ def tile_relativeglobalattention_pa_kernel(tc, q, k, inputV, Wv, E, out):
 
         q_raw = load_rows(nc, loads, q.flatten_outer_dims(), "q")
         e_raw = load_rows(nc, loads, E, "e")
+        k_raw = load_rows(nc, loads, k.flatten_outer_dims(), "k")
         x_raw = load_rows(nc, loads, inputV.flatten_outer_dims(), "x")
         w_raw = loads.tile([P, PACK * DV], BF16, name="w_raw")
         nc.sync.dma_start(
             out=w_raw[:].rearrange("p (u x) -> p u x", u=2),
             in_=Wv.rearrange("(u p h) c -> p u (h c)", u=2, h=2),
         )
-        k_raw = load_rows(nc, loads, k.flatten_outer_dims(), "k")
 
         ident_f32 = const.tile([P, P], F32, name="ident_f32")
         make_identity(nc, ident_f32[:])
@@ -99,14 +100,24 @@ def tile_relativeglobalattention_pa_kernel(tc, q, k, inputV, Wv, E, out):
         eT_pairs = eT[:].rearrange("p (c h) -> p c h", h=2)
         kT_pairs = kT[:].rearrange("p (c h) -> p c h", h=2)
 
+        w_grouped = keep.tile([P, PACK * DV], BF16, name="w_grouped", align_bytes=64)
+        w_codes = keep.tile([P, DV], U32, name="w_codes", align_bytes=64)
+        w_scales = keep.tile([P, DV], U8, name="w_scales", align_bytes=64)
+        x_grouped = keep.tile([P, PACK * L], BF16, name="x_grouped", align_bytes=64)
+        x_codes = keep.tile([P, L], U32, name="x_codes", align_bytes=64)
+        x_scales = keep.tile([P, L], U8, name="x_scales", align_bytes=64)
+        v_grouped = keep.tile([P, KEY_PASSES * PACK * DV], BF16, name="v_grouped", align_bytes=64)
+        v_codes = keep.tile([P, KEY_PASSES * DV], U32, name="v_codes", align_bytes=64)
+        v_scales = keep.tile([P, KEY_PASSES * DV], U8, name="v_scales", align_bytes=64)
+
         srel = {}
         shifts = {}
         e_rows = {}
         row_sums = {}
+        inverses = {}
         e_keys_first = {}
         e_quantised = {}
         sums = {}
-        inverses = {}
 
         def store_z(psum, i):
             z = z_pool.tile([P, Z_COLS], F32, name="z")
@@ -147,6 +158,70 @@ def tile_relativeglobalattention_pa_kernel(tc, q, k, inputV, Wv, E, out):
                 )[:, 0:L],
             )
             srel[i] = window
+
+        def group_w():
+            nc.vector.tensor_copy(
+                out=w_grouped[:].rearrange("p (c t) -> p c t", t=PACK),
+                in_=w_raw[:].rearrange("p (t c) -> p c t", t=PACK),
+            )
+
+        def quantise_w():
+            nc.vector.quantize_mx(out=w_codes[:].bitcast(FP8X4), scales=w_scales[:], in_=w_grouped[:])
+
+        def transpose_x(psum, b):
+            x_words = x_raw[:].bitcast(F32)
+            bank = psum.tile([P, BANK], F32, name="bank")
+            for s in range(X_KEYS // P):
+                t = b * (X_KEYS // P) + s
+                for u in range(2):
+                    nc.tensor.transpose(
+                        bank[:, u * X_KEYS + s * P : u * X_KEYS + (s + 1) * P],
+                        x_words[:, (2 * t + u) * P : (2 * t + u + 1) * P],
+                        ident_f32[:],
+                    )
+            copy_out(
+                nc,
+                b % 2 == 0,
+                x_grouped[:].bitcast(F32).rearrange("p (r u) -> p r u", u=2)[:, b * X_KEYS : (b + 1) * X_KEYS, :],
+                bank[:].rearrange("p (u r) -> p r u", u=2),
+            )
+
+        def quantise_x(b):
+            keys = slice(b * X_KEYS, (b + 1) * X_KEYS)
+            nc.vector.quantize_mx(
+                out=x_codes[:, keys].bitcast(FP8X4),
+                scales=x_scales[:, keys],
+                in_=x_grouped[:, b * X_KEYS * PACK : (b + 1) * X_KEYS * PACK],
+            )
+
+        def project_values(psum, g):
+            for c in range(DV // P):
+                bank = psum.tile([P, BANK], F32, name="bank")
+                for j in range(PACK):
+                    keys = slice((PACK * g + j) * P, (PACK * g + j + 1) * P)
+                    nc.tensor.matmul_mx(
+                        out=bank[:, j * P : (j + 1) * P],
+                        lhsT=x_codes[:, keys].bitcast(FP8X4),
+                        lhsT_scale=x_scales[:, keys],
+                        rhs=w_codes[:, c * P : (c + 1) * P].bitcast(FP8X4),
+                        rhs_scale=w_scales[:, c * P : (c + 1) * P],
+                        start=True,
+                        stop=True,
+                    )
+                first = (g * DV + c * P) * PACK
+                copy_out(
+                    nc,
+                    c % 2 == 0,
+                    v_grouped[:, first : first + P * PACK].rearrange("p (w j) -> p w j", j=PACK),
+                    bank[:].rearrange("p (j w) -> p w j", j=PACK),
+                )
+
+        def quantise_values(g):
+            nc.vector.quantize_mx(
+                out=v_codes[:, g * DV : (g + 1) * DV].bitcast(FP8X4),
+                scales=v_scales[:, g * DV : (g + 1) * DV],
+                in_=v_grouped[:, g * DV * PACK : (g + 1) * DV * PACK],
+            )
 
         def scores(psum, i):
             s = srel[i]
@@ -225,99 +300,28 @@ def tile_relativeglobalattention_pa_kernel(tc, q, k, inputV, Wv, E, out):
             nc.vector.memset(eT_words[:, 0:1], 0.0)
             transpose_pairs(nc, psum, ident_f32, q_raw, qT_words[:, 0:L], (True, True))
             transpose_pairs(nc, psum, ident_f32, e_raw, eT_words[:, 1 : L + 1], (False, False))
-
-            for i in range(SLOTS):
-                store_z(psum, i)
-            for i in range(SLOTS - 1):
-                read_windows(i)
-
-            w_grouped = keep.tile([P, PACK * DV], BF16, name="w_grouped", align_bytes=64)
-            w_codes = keep.tile([P, DV], U32, name="w_codes", align_bytes=64)
-            w_scales = keep.tile([P, DV], U8, name="w_scales", align_bytes=64)
-            nc.vector.tensor_copy(
-                out=w_grouped[:].rearrange("p (c t) -> p c t", t=PACK),
-                in_=w_raw[:].rearrange("p (t c) -> p c t", t=PACK),
-            )
-
-            x_grouped = keep.tile([P, PACK * L], BF16, name="x_grouped", align_bytes=64)
-            x_codes = keep.tile([P, L], U32, name="x_codes", align_bytes=64)
-            x_scales = keep.tile([P, L], U8, name="x_scales", align_bytes=64)
-            x_words = x_raw[:].bitcast(F32)
-            x_grouped_words = x_grouped[:].bitcast(F32).rearrange("p (r u) -> p r u", u=2)
-            keys_per_bank = BANK // 2
-
-            def quantise_x(b):
-                keys = slice(b * keys_per_bank, (b + 1) * keys_per_bank)
-                nc.vector.quantize_mx(
-                    out=x_codes[:, keys].bitcast(FP8X4),
-                    scales=x_scales[:, keys],
-                    in_=x_grouped[:, b * keys_per_bank * PACK : (b + 1) * keys_per_bank * PACK],
-                )
-
-            for b in range(L // keys_per_bank):
-                bank = psum.tile([P, BANK], F32, name="bank")
-                for s in range(keys_per_bank // P):
-                    t = b * (keys_per_bank // P) + s
-                    for u in range(2):
-                        nc.tensor.transpose(
-                            bank[:, u * keys_per_bank + s * P : u * keys_per_bank + (s + 1) * P],
-                            x_words[:, (2 * t + u) * P : (2 * t + u + 1) * P],
-                            ident_f32[:],
-                        )
-                copy_out(
-                    nc,
-                    b % 2 == 0,
-                    x_grouped_words[:, b * keys_per_bank : (b + 1) * keys_per_bank, :],
-                    bank[:].rearrange("p (u r) -> p r u", u=2),
-                )
-                if b == 0:
-                    nc.vector.quantize_mx(out=w_codes[:].bitcast(FP8X4), scales=w_scales[:], in_=w_grouped[:])
-                if b >= 1:
-                    quantise_x(b - 1)
-            quantise_x(L // keys_per_bank - 1)
-            transpose_pairs(nc, psum, ident_f32, k_raw, kT[:].bitcast(F32), (True, False))
-
-            v_grouped = keep.tile([P, KEY_PASSES * PACK * DV], BF16, name="v_grouped", align_bytes=64)
-            v_codes = keep.tile([P, KEY_PASSES * DV], U32, name="v_codes", align_bytes=64)
-            v_scales = keep.tile([P, KEY_PASSES * DV], U8, name="v_scales", align_bytes=64)
-
-            def project_values(psum, g):
-                for c in range(DV // P):
-                    bank = psum.tile([P, BANK], F32, name="bank")
-                    for j in range(PACK):
-                        keys = slice((PACK * g + j) * P, (PACK * g + j + 1) * P)
-                        nc.tensor.matmul_mx(
-                            out=bank[:, j * P : (j + 1) * P],
-                            lhsT=x_codes[:, keys].bitcast(FP8X4),
-                            lhsT_scale=x_scales[:, keys],
-                            rhs=w_codes[:, c * P : (c + 1) * P].bitcast(FP8X4),
-                            rhs_scale=w_scales[:, c * P : (c + 1) * P],
-                            start=True,
-                            stop=True,
-                        )
-                    first = (g * DV + c * P) * PACK
-                    nc.scalar.copy(
-                        out=v_grouped[:, first : first + P * PACK].rearrange("p (w j) -> p w j", j=PACK),
-                        in_=bank[:].rearrange("p (j w) -> p w j", j=PACK),
-                    )
-
-            def quantise_values(g):
-                nc.vector.quantize_mx(
-                    out=v_codes[:, g * DV : (g + 1) * DV].bitcast(FP8X4),
-                    scales=v_scales[:, g * DV : (g + 1) * DV],
-                    in_=v_grouped[:, g * DV * PACK : (g + 1) * DV * PACK],
-                )
-
-            store_z(psum, SLOTS)
-            read_windows(SLOTS - 1)
-            project_values(psum, 0)
+            transpose_pairs(nc, psum, ident_f32, k_raw, kT[:].bitcast(F32), (True, True))
+            store_z(psum, 0)
+            group_w()
+            for b in range(L // X_KEYS):
+                transpose_x(psum, b)
+            quantise_w()
+            store_z(psum, 1)
+            read_windows(0)
+            for b in range(L // X_KEYS):
+                quantise_x(b)
+            store_z(psum, 2)
+            read_windows(1)
+            for g in range(KEY_PASSES):
+                project_values(psum, g)
+            store_z(psum, 3)
+            read_windows(2)
 
         assert P * DV <= FIRST_SLOT
         with ExitStack() as banks:
-            psum_z = banks.enter_context(tc.psum_pool(name="psum_z", bufs=3))
+            psum_zo = banks.enter_context(tc.psum_pool(name="psum_zo", bufs=4))
             psum_s = banks.enter_context(tc.psum_pool(name="psum_s", bufs=2))
             psum_e = banks.enter_context(tc.psum_pool(name="psum_e", bufs=2))
-            psum_o = banks.enter_context(tc.psum_pool(name="psum_o", bufs=1))
             for n in range(TILES + 3):
                 if 0 <= n - 1 < TILES:
                     exponentials(n - 1)
@@ -326,13 +330,11 @@ def tile_relativeglobalattention_pa_kernel(tc, q, k, inputV, Wv, E, out):
                 if n < KEY_PASSES:
                     quantise_values(n)
                 if n + SLOTS + 1 < TILES:
-                    store_z(psum_z, n + SLOTS + 1)
+                    store_z(psum_zo, n + SLOTS + 1)
                 if n + SLOTS < TILES:
                     read_windows(n + SLOTS)
                 if 0 <= n - 3 < TILES:
-                    multiply_e_v(psum_o, n - 3)
-                if n == 0:
-                    project_values(psum_e, 1)
+                    multiply_e_v(psum_zo, n - 3)
                 if 0 <= n - 1 < TILES:
                     transpose_e(psum_e, n - 1)
                 if 0 <= n - 2 < TILES:

@@ -19,7 +19,7 @@ L, DK, D, DV = 1024, 256, 512, 512
 TILES = L // P
 KEY_PASSES = L // (P * PACK)
 X_KEYS = BANK // 2
-SCALE = 1.0 / 16.0
+NEGATED_SCALE = -1.0 / 16.0
 
 Z_COLS = L + P
 SLOTS = 3
@@ -33,6 +33,13 @@ def copy_out(nc, on_scalar, out, in_):
         nc.scalar.copy(out=out, in_=in_)
     else:
         nc.vector.tensor_copy(out=out, in_=in_)
+
+
+def scaled_copy_out(nc, on_scalar, out, in_, factor):
+    if on_scalar:
+        nc.scalar.activation(out=out, in_=in_, func=ACT.Copy, scale=factor)
+    else:
+        nc.vector.tensor_scalar_mul(out=out, in0=in_, scalar1=factor)
 
 
 def load_rows(nc, pool, src, label):
@@ -71,8 +78,8 @@ def tile_relativeglobalattention_pa_kernel(tc, q, k, inputV, Wv, E, out):
         small = ctx.enter_context(tc.tile_pool(name="small", bufs=5))
         results = ctx.enter_context(tc.tile_pool(name="results", bufs=4))
 
-        q_raw = load_rows(nc, loads, q.flatten_outer_dims(), "q")
         e_raw = load_rows(nc, loads, E, "e")
+        q_raw = load_rows(nc, loads, q.flatten_outer_dims(), "q")
         k_raw = load_rows(nc, loads, k.flatten_outer_dims(), "k")
         x_raw = load_rows(nc, loads, inputV.flatten_outer_dims(), "x")
         w_raw = loads.tile([P, PACK * DV], BF16, name="w_raw")
@@ -110,7 +117,7 @@ def tile_relativeglobalattention_pa_kernel(tc, q, k, inputV, Wv, E, out):
         v_codes = keep.tile([P, KEY_PASSES * DV], U32, name="v_codes", align_bytes=64)
         v_scales = keep.tile([P, KEY_PASSES * DV], U8, name="v_scales", align_bytes=64)
 
-        srel = {}
+        logits = {}
         shifts = {}
         e_rows = {}
         row_sums = {}
@@ -140,7 +147,7 @@ def tile_relativeglobalattention_pa_kernel(tc, q, k, inputV, Wv, E, out):
                             start=(h == 0),
                             stop=(h == 1),
                         )
-                    copy_out(nc, piece != 1, z[:, z_first + c : z_first + c + n], bank[:, :n])
+                    scaled_copy_out(nc, piece != 1, z[:, z_first + c : z_first + c + n], bank[:, :n], NEGATED_SCALE)
                     piece += 1
             base = FIRST_SLOT + (i % SLOTS) * P * Z_COLS
             nc.sync.dma_start(
@@ -157,12 +164,16 @@ def tile_relativeglobalattention_pa_kernel(tc, q, k, inputV, Wv, E, out):
                     "(p t) -> p t", t=Z_COLS - 1
                 )[:, 0:L],
             )
-            srel[i] = window
+            logits[i] = window
 
         def group_w():
-            nc.vector.tensor_copy(
+            nc.gpsimd.tensor_scalar(
                 out=w_grouped[:].rearrange("p (c t) -> p c t", t=PACK),
-                in_=w_raw[:].rearrange("p (t c) -> p c t", t=PACK),
+                in0=w_raw[:].rearrange("p (t c) -> p c t", t=PACK),
+                scalar1=1.0,
+                scalar2=0.0,
+                op0=ALU.mult,
+                op1=ALU.add,
             )
 
         def quantise_w():
@@ -224,7 +235,7 @@ def tile_relativeglobalattention_pa_kernel(tc, q, k, inputV, Wv, E, out):
             )
 
         def scores(psum, i):
-            s = srel[i]
+            t = logits[i]
             for half in range(L // BANK):
                 cols = slice(half * BANK, (half + 1) * BANK)
                 bank = psum.tile([P, BANK], F32, name="bank")
@@ -236,18 +247,18 @@ def tile_relativeglobalattention_pa_kernel(tc, q, k, inputV, Wv, E, out):
                         start=(h == 0),
                         stop=(h == 1),
                     )
-                nc.vector.tensor_tensor(out=s[:, cols], in0=bank[:], in1=s[:, cols], op=ALU.add)
-            row_max = small.tile([P, 1], F32, name="row_max")
-            nc.vector.reduce_max(out=row_max[:], in_=s[:], axis=AXIS.X)
+                nc.vector.scalar_tensor_tensor(
+                    out=t[:, cols], in0=bank[:], scalar=NEGATED_SCALE, in1=t[:, cols], op0=ALU.mult, op1=ALU.add
+                )
             shift = small.tile([P, 1], F32, name="shift")
-            nc.vector.tensor_scalar_mul(out=shift[:], in0=row_max[:], scalar1=-SCALE)
+            nc.vector.tensor_reduce(out=shift[:], in_=t[:], axis=AXIS.X, op=ALU.min)
             shifts[i] = shift
 
         def exponentials(i):
             e_bf16 = work.tile([P, L], BF16, name="e_bf16")
             row_sum = small.tile([P, 1], F32, name="row_sum")
             nc.scalar.activation(
-                out=e_bf16[:], in_=srel[i][:], func=ACT.Exp, bias=shifts[i][:], scale=SCALE, accum_out=row_sum[:]
+                out=e_bf16[:], in_=logits[i][:], func=ACT.Exp, bias=shifts[i][:], scale=-1.0, accum_out=row_sum[:]
             )
             e_rows[i] = e_bf16
             row_sums[i] = row_sum
@@ -298,24 +309,24 @@ def tile_relativeglobalattention_pa_kernel(tc, q, k, inputV, Wv, E, out):
         with tc.psum_pool(name="psum_head", bufs=8) as psum:
             nc.vector.memset(qT_words[:, L : L + 1], 0.0)
             nc.vector.memset(eT_words[:, 0:1], 0.0)
-            transpose_pairs(nc, psum, ident_f32, q_raw, qT_words[:, 0:L], (True, True))
             transpose_pairs(nc, psum, ident_f32, e_raw, eT_words[:, 1 : L + 1], (False, False))
-            transpose_pairs(nc, psum, ident_f32, k_raw, kT[:].bitcast(F32), (True, True))
+            transpose_pairs(nc, psum, ident_f32, q_raw, qT_words[:, 0:L], (True, True))
             store_z(psum, 0)
-            group_w()
-            for b in range(L // X_KEYS):
-                transpose_x(psum, b)
-            quantise_w()
             store_z(psum, 1)
             read_windows(0)
-            for b in range(L // X_KEYS):
-                quantise_x(b)
             store_z(psum, 2)
             read_windows(1)
-            for g in range(KEY_PASSES):
-                project_values(psum, g)
+            transpose_pairs(nc, psum, ident_f32, k_raw, kT[:].bitcast(F32), (True, True))
+            for b in range(L // X_KEYS):
+                transpose_x(psum, b)
+            group_w()
+            quantise_w()
+            for b in range(L // X_KEYS):
+                quantise_x(b)
             store_z(psum, 3)
             read_windows(2)
+            for g in range(KEY_PASSES):
+                project_values(psum, g)
 
         assert P * DV <= FIRST_SLOT
         with ExitStack() as banks:

@@ -80,13 +80,13 @@ def tile_relativeglobalattention_pa_kernel(tc, q, k, inputV, Wv, E, out):
 
         e_raw = load_rows(nc, loads, E, "e")
         q_raw = load_rows(nc, loads, q.flatten_outer_dims(), "q")
-        k_raw = load_rows(nc, loads, k.flatten_outer_dims(), "k")
-        x_raw = load_rows(nc, loads, inputV.flatten_outer_dims(), "x")
         w_raw = loads.tile([P, PACK * DV], BF16, name="w_raw")
         nc.sync.dma_start(
             out=w_raw[:].rearrange("p (u x) -> p u x", u=2),
             in_=Wv.rearrange("(u p h) c -> p u (h c)", u=2, h=2),
         )
+        k_raw = load_rows(nc, loads, k.flatten_outer_dims(), "k")
+        x_raw = load_rows(nc, loads, inputV.flatten_outer_dims(), "x")
 
         ident_f32 = const.tile([P, P], F32, name="ident_f32")
         make_identity(nc, ident_f32[:])
@@ -298,9 +298,9 @@ def tile_relativeglobalattention_pa_kernel(tc, q, k, inputV, Wv, E, out):
                 )
             sums[i] = acc
 
-        def normalise_and_store(i):
+        def normalise_and_store(i, on_scalar):
             result = results.tile([P, DV], F32, name="result")
-            if i % 2 == 0:
+            if on_scalar:
                 nc.scalar.activation(out=result[:], in_=sums[i][:], func=ACT.Copy, scale=inverses[i][:])
             else:
                 nc.vector.tensor_scalar_mul(out=result[:], in0=sums[i][:], scalar1=inverses[i][:])
@@ -312,15 +312,15 @@ def tile_relativeglobalattention_pa_kernel(tc, q, k, inputV, Wv, E, out):
             transpose_pairs(nc, psum, ident_f32, e_raw, eT_words[:, 1 : L + 1], (False, False))
             transpose_pairs(nc, psum, ident_f32, q_raw, qT_words[:, 0:L], (True, True))
             store_z(psum, 0)
+            group_w()
             store_z(psum, 1)
             read_windows(0)
             store_z(psum, 2)
             read_windows(1)
+            quantise_w()
             transpose_pairs(nc, psum, ident_f32, k_raw, kT[:].bitcast(F32), (True, True))
             for b in range(L // X_KEYS):
                 transpose_x(psum, b)
-            group_w()
-            quantise_w()
             for b in range(L // X_KEYS):
                 quantise_x(b)
             store_z(psum, 3)
@@ -351,4 +351,4 @@ def tile_relativeglobalattention_pa_kernel(tc, q, k, inputV, Wv, E, out):
                 if 0 <= n - 2 < TILES:
                     quantise_e(n - 2)
                 if 0 <= n - 3 < TILES:
-                    normalise_and_store(n - 3)
+                    normalise_and_store(n - 3, n < TILES)

@@ -17,6 +17,7 @@ PACK = 4
 BANK = 512
 L, DK, D, DV = 1024, 256, 512, 512
 TILES = L // P
+HALVES = L // BANK
 KEY_PASSES = L // (P * PACK)
 X_KEYS = BANK // 2
 NEGATED_SCALE = -1.0 / 16.0
@@ -25,87 +26,95 @@ Z_COLS = L + P
 SLOTS = 3
 FIRST_SLOT = L * DV - SLOTS * P * Z_COLS
 
+S, V = "scalar", "vector"
+QK_BANKS = 4
+LAG = 3
+
 FLOPS = 2 * L * (D * DV + 2 * L * DK + L * DV)
 
 
-def copy_out(nc, on_scalar, out, in_):
-    if on_scalar:
+def copy_out(nc, engine, out, in_):
+    if engine == S:
         nc.scalar.copy(out=out, in_=in_)
     else:
         nc.vector.tensor_copy(out=out, in_=in_)
 
 
-def scaled_copy_out(nc, on_scalar, out, in_, factor):
-    if on_scalar:
+def scaled_copy_out(nc, engine, out, in_, factor):
+    if engine == S:
         nc.scalar.activation(out=out, in_=in_, func=ACT.Copy, scale=factor)
     else:
         nc.vector.tensor_scalar_mul(out=out, in0=in_, scalar1=factor)
 
 
-def load_rows(nc, pool, src, label):
-    width = src.shape[1]
-    raw = pool.tile([P, TILES * width], BF16, name="%s_raw" % label)
-    nc.sync.dma_start(
-        out=raw[:].rearrange("p (t d) -> p t d", t=TILES),
-        in_=src.rearrange("(t p) d -> p t d", p=P),
-    )
-    return raw
-
-
-def transpose_pairs(nc, psum, ident_f32, raw, dst_words, on_scalar):
-    raw_words = raw[:].bitcast(F32)
-    for half in range(L // BANK):
-        bank = psum.tile([P, BANK], F32, name="bank")
-        for s in range(BANK // P):
-            t = half * (BANK // P) + s
-            nc.tensor.transpose(bank[:, s * P : (s + 1) * P], raw_words[:, t * P : (t + 1) * P], ident_f32[:])
-        copy_out(nc, on_scalar[half], dst_words[:, half * BANK : (half + 1) * BANK], bank[:])
-
-
 def tile_relativeglobalattention_pa_kernel(tc, q, k, inputV, Wv, E, out):
     nc = tc.nc
-    out_rows = out.flatten_outer_dims()
+    q_rows, k_rows, x_rows, out_rows = (a.flatten_outer_dims() for a in (q, k, inputV, out))
     out_flat = out.rearrange("b l d -> (b l d)")
 
     with ExitStack() as ctx:
         ctx.enter_context(tc.manual_schedule())
         const = ctx.enter_context(tc.tile_pool(name="const", bufs=1))
-        loads = ctx.enter_context(tc.tile_pool(name="loads", bufs=1))
         keep = ctx.enter_context(tc.tile_pool(name="keep", bufs=1))
         z_pool = ctx.enter_context(tc.tile_pool(name="z", bufs=5))
         s_pool = ctx.enter_context(tc.tile_pool(name="s", bufs=TILES))
-        work = ctx.enter_context(tc.tile_pool(name="work", bufs=3))
-        small = ctx.enter_context(tc.tile_pool(name="small", bufs=5))
-        results = ctx.enter_context(tc.tile_pool(name="results", bufs=4))
+        work = ctx.enter_context(tc.tile_pool(name="work", bufs=5))
+        small = ctx.enter_context(tc.tile_pool(name="small", bufs=8))
+        results = ctx.enter_context(tc.tile_pool(name="results", bufs=TILES + 1))
+        psum = ctx.enter_context(tc.psum_pool(name="psum", bufs=8 - QK_BANKS))
+        psum_qk = ctx.enter_context(tc.psum_pool(name="psum_qk", bufs=QK_BANKS))
 
-        e_raw = load_rows(nc, loads, E, "e")
-        q_raw = load_rows(nc, loads, q.flatten_outer_dims(), "q")
-        w_raw = loads.tile([P, PACK * DV], BF16, name="w_raw")
+        def load_chunk(name, src, first, slots):
+            chunk = keep.tile([P, slots * DK], BF16, name="%s_raw%d" % (name, first))
+            nc.sync.dma_start(
+                out=chunk[:],
+                in_=src[first : first + slots * P, :].rearrange("(p t) d -> p (t d)", t=slots),
+            )
+            raw[name, first] = (chunk, slots)
+
+        raw = {}
+        load_chunk("q", q_rows, 0, 2)
+        for quarter in range(4):
+            load_chunk("e", E, 256 * quarter, 2)
+        load_chunk("q", q_rows, 256, 2)
+
+        w_raw = keep.tile([P, PACK * DV], BF16, name="w_raw")
         nc.sync.dma_start(
             out=w_raw[:].rearrange("p (u x) -> p u x", u=2),
             in_=Wv.rearrange("(u p h) c -> p u (h c)", u=2, h=2),
         )
-        k_raw = load_rows(nc, loads, k.flatten_outer_dims(), "k")
-        x_raw = load_rows(nc, loads, inputV.flatten_outer_dims(), "x")
+        x_raw = keep.tile([P, TILES * D], BF16, name="x_raw")
+
+        def load_x(half):
+            nc.sync.dma_start(
+                out=x_raw[:].rearrange("p (s x) -> p s x", s=PACK)[:, 2 * half : 2 * half + 2, :],
+                in_=x_rows[half * BANK : (half + 1) * BANK, :].rearrange("(s p h) d -> p s (h d)", p=P, h=2),
+            )
+
+        load_x(0)
+        load_chunk("k", k_rows, 0, 4)
+        load_chunk("k", k_rows, 512, 4)
+        load_x(1)
+        load_chunk("q", q_rows, 512, 4)
 
         ident_f32 = const.tile([P, P], F32, name="ident_f32")
         make_identity(nc, ident_f32[:])
-        ident_bf16 = const.tile([P, P], BF16, name="ident_bf16")
-        make_identity(nc, ident_bf16[:])
 
         zero = const.tile([P, 1], F32, name="zero")
         one = const.tile([P, 1], F32, name="one")
         nc.vector.memset(zero[:], 0.0)
         nc.scalar.activation(out=one[:], in_=zero[:], func=ACT.Exp)
 
+        E_FIRST = PACK
         qT = keep.tile([P, 2 * (L + 1)], BF16, name="qT")
-        eT = keep.tile([P, 2 * (L + 1)], BF16, name="eT")
+        eT = keep.tile([P, 2 * (L + E_FIRST)], BF16, name="eT")
         kT = keep.tile([P, 2 * L], BF16, name="kT")
-        qT_words = qT[:].bitcast(F32)
-        eT_words = eT[:].bitcast(F32)
+        transposed = {"q": (qT, 0), "e": (eT, E_FIRST), "k": (kT, 0)}
         qT_pairs = qT[:].rearrange("p (c h) -> p c h", h=2)
         eT_pairs = eT[:].rearrange("p (c h) -> p c h", h=2)
         kT_pairs = kT[:].rearrange("p (c h) -> p c h", h=2)
+        nc.vector.memset(qT[:].bitcast(F32)[:, L : L + 1], 0.0)
+        nc.vector.memset(eT[:].bitcast(F32)[:, 0:E_FIRST], 0.0)
 
         w_grouped = keep.tile([P, PACK * DV], BF16, name="w_grouped", align_bytes=64)
         w_codes = keep.tile([P, DV], U32, name="w_codes", align_bytes=64)
@@ -117,42 +126,53 @@ def tile_relativeglobalattention_pa_kernel(tc, q, k, inputV, Wv, E, out):
         v_codes = keep.tile([P, KEY_PASSES * DV], U32, name="v_codes", align_bytes=64)
         v_scales = keep.tile([P, KEY_PASSES * DV], U8, name="v_scales", align_bytes=64)
 
-        logits = {}
-        shifts = {}
-        e_rows = {}
-        row_sums = {}
-        inverses = {}
-        e_keys_first = {}
-        e_quantised = {}
-        sums = {}
+        z_tiles, logits, qk, shifts, e_rows, row_sums, inverses, e_keys_first, e_grouped, e_quantised, sums = (
+            {} for stage in range(11)
+        )
 
-        def store_z(psum, i):
-            z = z_pool.tile([P, Z_COLS], F32, name="z")
-            first_part = (i + 1) * P
-            parts = (
-                (0, 1 + L - first_part, first_part, 0),
-                (1, 0, Z_COLS - first_part, first_part),
+        def transpose_chunk(name, first, engine):
+            dst, offset = transposed[name]
+            chunk, slots = raw[name, first]
+            words = chunk[:].bitcast(F32)
+            bank = psum.tile([P, BANK], F32, name="bank")
+            for t in range(slots):
+                nc.tensor.transpose(bank[:, t * P : (t + 1) * P], words[:, t * P : (t + 1) * P], ident_f32[:])
+            columns = slice(offset + first, offset + first + slots * P)
+            copy_out(
+                nc,
+                engine,
+                dst[:].bitcast(F32)[:, columns].rearrange("p (r t) -> p r t", t=slots),
+                bank[:, : slots * P].rearrange("p (t r) -> p r t", t=slots),
             )
-            piece = 0
-            for next_query, e_first, width, z_first in parts:
+
+        def z_piece(i, z_first, width, engine):
+            if i not in z_tiles:
+                z_tiles[i] = z_pool.tile([P, Z_COLS], F32, name="z")
+            first_part = (i + 1) * P
+            bank = psum.tile([P, BANK], F32, name="bank")
+            spans = (
+                (0, z_first, min(z_first + width, first_part), E_FIRST + L - first_part),
+                (1, max(z_first, first_part), z_first + width, E_FIRST - 1 - first_part),
+            )
+            for next_query, begin, end, e_offset in spans:
+                if begin >= end:
+                    continue
                 queries = slice(i * P + next_query, (i + 1) * P + next_query)
-                for c in range(0, width, BANK):
-                    n = min(BANK, width - c)
-                    bank = psum.tile([P, BANK], F32, name="bank")
-                    for h in range(2):
-                        nc.tensor.matmul(
-                            out=bank[:, :n],
-                            lhsT=qT_pairs[:, queries, h],
-                            rhs=eT_pairs[:, e_first + c : e_first + c + n, h],
-                            start=(h == 0),
-                            stop=(h == 1),
-                        )
-                    scaled_copy_out(nc, piece != 1, z[:, z_first + c : z_first + c + n], bank[:, :n], NEGATED_SCALE)
-                    piece += 1
+                for h in range(2):
+                    nc.tensor.matmul(
+                        out=bank[:, begin - z_first : end - z_first],
+                        lhsT=qT_pairs[:, queries, h],
+                        rhs=eT_pairs[:, e_offset + begin : e_offset + end, h],
+                        start=(h == 0),
+                        stop=(h == 1),
+                    )
+            scaled_copy_out(nc, engine, z_tiles[i][:, z_first : z_first + width], bank[:, :width], NEGATED_SCALE)
+
+        def store_z(i):
             base = FIRST_SLOT + (i % SLOTS) * P * Z_COLS
             nc.sync.dma_start(
                 out=out_flat[base : base + P * Z_COLS].rearrange("(p t) -> p t", t=Z_COLS),
-                in_=z[:],
+                in_=z_tiles[i][:],
             )
 
         def read_windows(i):
@@ -179,7 +199,7 @@ def tile_relativeglobalattention_pa_kernel(tc, q, k, inputV, Wv, E, out):
         def quantise_w():
             nc.vector.quantize_mx(out=w_codes[:].bitcast(FP8X4), scales=w_scales[:], in_=w_grouped[:])
 
-        def transpose_x(psum, b):
+        def transpose_x(b, engine):
             x_words = x_raw[:].bitcast(F32)
             bank = psum.tile([P, BANK], F32, name="bank")
             for s in range(X_KEYS // P):
@@ -192,7 +212,7 @@ def tile_relativeglobalattention_pa_kernel(tc, q, k, inputV, Wv, E, out):
                     )
             copy_out(
                 nc,
-                b % 2 == 0,
+                engine,
                 x_grouped[:].bitcast(F32).rearrange("p (r u) -> p r u", u=2)[:, b * X_KEYS : (b + 1) * X_KEYS, :],
                 bank[:].rearrange("p (u r) -> p r u", u=2),
             )
@@ -205,27 +225,26 @@ def tile_relativeglobalattention_pa_kernel(tc, q, k, inputV, Wv, E, out):
                 in_=x_grouped[:, b * X_KEYS * PACK : (b + 1) * X_KEYS * PACK],
             )
 
-        def project_values(psum, g):
-            for c in range(DV // P):
-                bank = psum.tile([P, BANK], F32, name="bank")
-                for j in range(PACK):
-                    keys = slice((PACK * g + j) * P, (PACK * g + j + 1) * P)
-                    nc.tensor.matmul_mx(
-                        out=bank[:, j * P : (j + 1) * P],
-                        lhsT=x_codes[:, keys].bitcast(FP8X4),
-                        lhsT_scale=x_scales[:, keys],
-                        rhs=w_codes[:, c * P : (c + 1) * P].bitcast(FP8X4),
-                        rhs_scale=w_scales[:, c * P : (c + 1) * P],
-                        start=True,
-                        stop=True,
-                    )
-                first = (g * DV + c * P) * PACK
-                copy_out(
-                    nc,
-                    c % 2 == 0,
-                    v_grouped[:, first : first + P * PACK].rearrange("p (w j) -> p w j", j=PACK),
-                    bank[:].rearrange("p (j w) -> p w j", j=PACK),
+        def project_values(g, c, engine):
+            bank = psum.tile([P, BANK], F32, name="bank")
+            for j in range(PACK):
+                keys = slice((PACK * g + j) * P, (PACK * g + j + 1) * P)
+                nc.tensor.matmul_mx(
+                    out=bank[:, j * P : (j + 1) * P],
+                    lhsT=x_codes[:, keys].bitcast(FP8X4),
+                    lhsT_scale=x_scales[:, keys],
+                    rhs=w_codes[:, c * P : (c + 1) * P].bitcast(FP8X4),
+                    rhs_scale=w_scales[:, c * P : (c + 1) * P],
+                    start=True,
+                    stop=True,
                 )
+            first = (g * DV + c * P) * PACK
+            copy_out(
+                nc,
+                engine,
+                v_grouped[:, first : first + P * PACK].rearrange("p (w j) -> p w j", j=PACK),
+                bank[:].rearrange("p (j w) -> p w j", j=PACK),
+            )
 
         def quantise_values(g):
             nc.vector.quantize_mx(
@@ -234,61 +253,95 @@ def tile_relativeglobalattention_pa_kernel(tc, q, k, inputV, Wv, E, out):
                 in_=v_grouped[:, g * DV * PACK : (g + 1) * DV * PACK],
             )
 
-        def scores(psum, i):
-            t = logits[i]
-            for half in range(L // BANK):
-                cols = slice(half * BANK, (half + 1) * BANK)
-                bank = psum.tile([P, BANK], F32, name="bank")
-                for h in range(2):
-                    nc.tensor.matmul(
-                        out=bank[:],
-                        lhsT=qT_pairs[:, i * P : (i + 1) * P, h],
-                        rhs=kT_pairs[:, cols, h],
-                        start=(h == 0),
-                        stop=(h == 1),
-                    )
-                nc.vector.scalar_tensor_tensor(
-                    out=t[:, cols], in0=bank[:], scalar=NEGATED_SCALE, in1=t[:, cols], op0=ALU.mult, op1=ALU.add
+        def multiply_qk(i, half):
+            cols = slice(half * BANK, (half + 1) * BANK)
+            bank = psum_qk.tile([P, BANK], F32, name="bank")
+            for h in range(2):
+                nc.tensor.matmul(
+                    out=bank[:],
+                    lhsT=qT_pairs[:, i * P : (i + 1) * P, h],
+                    rhs=kT_pairs[:, cols, h],
+                    start=(h == 0),
+                    stop=(h == 1),
                 )
+            qk[i, half] = bank
+
+        def add_scores(i, half):
+            cols = slice(half * BANK, (half + 1) * BANK)
+            t = logits[i]
+            nc.vector.scalar_tensor_tensor(
+                out=t[:, cols], in0=qk[i, half][:], scalar=NEGATED_SCALE, in1=t[:, cols], op0=ALU.mult, op1=ALU.add
+            )
+
+        def row_minimum(i):
             shift = small.tile([P, 1], F32, name="shift")
-            nc.vector.tensor_reduce(out=shift[:], in_=t[:], axis=AXIS.X, op=ALU.min)
+            nc.vector.tensor_reduce(out=shift[:], in_=logits[i][:], axis=AXIS.X, op=ALU.min)
             shifts[i] = shift
 
-        def exponentials(i):
-            e_bf16 = work.tile([P, L], BF16, name="e_bf16")
-            row_sum = small.tile([P, 1], F32, name="row_sum")
+        def exponentials(i, begin=0, end=KEY_PASSES):
+            if begin == 0:
+                e_rows[i] = work.tile([P, L], BF16, name="e_bf16")
+                row_sums[i] = []
+            row_sum = small.tile([P, 1], F32, name="row_sum%d" % begin)
+            cols = slice(begin * BANK, end * BANK)
             nc.scalar.activation(
-                out=e_bf16[:], in_=logits[i][:], func=ACT.Exp, bias=shifts[i][:], scale=-1.0, accum_out=row_sum[:]
+                out=e_rows[i][:, cols],
+                in_=logits[i][:, cols],
+                func=ACT.Exp,
+                bias=shifts[i][:],
+                scale=-1.0,
+                accum_out=row_sum[:],
             )
-            e_rows[i] = e_bf16
-            row_sums[i] = row_sum
+            row_sums[i].append(row_sum)
 
-        def transpose_e(psum, i):
-            bank = psum.tile([P, L], BF16, name="bank")
-            for t in range(TILES):
-                nc.tensor.transpose(bank[:, t * P : (t + 1) * P], e_rows[i][:, t * P : (t + 1) * P], ident_bf16[:])
-            e_keys_first[i] = bank
+        def transpose_e(i, begin=0, end=KEY_PASSES):
+            e_words = e_rows[i][:].bitcast(F32)
+            bank = psum.tile([P, BANK], F32, name="bank")
+            for s in range(2 * begin, 2 * end):
+                nc.tensor.transpose(
+                    bank[:, (s - 2 * begin) * P : (s - 2 * begin + 1) * P], e_words[:, s * P : (s + 1) * P], ident_f32[:]
+                )
+            e_keys_first[i, begin] = bank
 
-        def quantise_e(i):
+        def group_e(i, engine, begin=0, end=KEY_PASSES):
+            if begin == 0:
+                e_grouped[i] = work.tile([P, L], BF16, name="e_grouped", align_bytes=64)
+            copy_out(
+                nc,
+                engine,
+                e_grouped[i][:].bitcast(F32).rearrange("p (g w u) -> p g w u", g=KEY_PASSES, u=2)[:, begin:end],
+                e_keys_first[i, begin][:, : (end - begin) * 2 * P].rearrange("p (g u w) -> p g w u", u=2, w=P),
+            )
+
+        def invert_row_sum(i):
             inverse = small.tile([P, 1], F32, name="inverse")
-            nc.vector.reciprocal(out=inverse[:], in_=row_sums[i][:])
+            total = row_sums[i][0]
+            if len(row_sums[i]) > 1:
+                total = small.tile([P, 1], F32, name="total")
+                nc.vector.tensor_tensor(out=total[:], in0=row_sums[i][0][:], in1=row_sums[i][1][:], op=ALU.add)
+            nc.vector.reciprocal(out=inverse[:], in_=total[:])
             inverses[i] = inverse
-            e_grouped = work.tile([P, L], BF16, name="e_grouped", align_bytes=64)
-            nc.scalar.copy(
-                out=e_grouped[:].rearrange("p (g w j) -> p g w j", g=KEY_PASSES, j=PACK),
-                in_=e_keys_first[i][:].rearrange("p (g j w) -> p g w j", g=KEY_PASSES, j=PACK),
-            )
-            e_codes = work.tile([P, KEY_PASSES * P], U32, name="e_codes", align_bytes=64)
-            e_scales = work.tile([P, KEY_PASSES * P], U8, name="e_scales", align_bytes=64)
-            nc.vector.quantize_mx(out=e_codes[:].bitcast(FP8X4), scales=e_scales[:], in_=e_grouped[:])
-            e_quantised[i] = (e_codes, e_scales)
 
-        def multiply_e_v(psum, i):
+        def quantise_e(i, begin=0, end=KEY_PASSES):
+            if begin == 0:
+                e_codes = work.tile([P, KEY_PASSES * P], U32, name="e_codes", align_bytes=64)
+                e_scales = work.tile([P, KEY_PASSES * P], U8, name="e_scales", align_bytes=64)
+                e_quantised[i] = (e_codes, e_scales)
             e_codes, e_scales = e_quantised[i]
-            acc = psum.tile([P, DV], F32, name="bank")
-            for g in range(KEY_PASSES):
+            words = slice(begin * P, end * P)
+            nc.vector.quantize_mx(
+                out=e_codes[:, words].bitcast(FP8X4),
+                scales=e_scales[:, words],
+                in_=e_grouped[i][:, begin * BANK : end * BANK],
+            )
+
+        def multiply_e_v(i, begin=0, end=KEY_PASSES):
+            e_codes, e_scales = e_quantised[i]
+            if begin == 0:
+                sums[i] = psum.tile([P, DV], F32, name="bank")
+            for g in range(begin, end):
                 nc.tensor.matmul_mx(
-                    out=acc[:],
+                    out=sums[i][:],
                     lhsT=e_codes[:, g * P : (g + 1) * P].bitcast(FP8X4),
                     lhsT_scale=e_scales[:, g * P : (g + 1) * P],
                     rhs=v_codes[:, g * DV : (g + 1) * DV].bitcast(FP8X4),
@@ -296,59 +349,109 @@ def tile_relativeglobalattention_pa_kernel(tc, q, k, inputV, Wv, E, out):
                     start=(g == 0),
                     stop=(g == KEY_PASSES - 1),
                 )
-            sums[i] = acc
 
-        def normalise_and_store(i, on_scalar):
+        def normalise_and_store(i, *engines):
             result = results.tile([P, DV], F32, name="result")
-            if on_scalar:
-                nc.scalar.activation(out=result[:], in_=sums[i][:], func=ACT.Copy, scale=inverses[i][:])
-            else:
-                nc.vector.tensor_scalar_mul(out=result[:], in0=sums[i][:], scalar1=inverses[i][:])
+            width = DV // len(engines)
+            for share, engine in enumerate(engines):
+                cols = slice(share * width, (share + 1) * width)
+                scaled_copy_out(nc, engine, result[:, cols], sums[i][:, cols], inverses[i][:])
             nc.sync.dma_start(out=out_rows[i * P : (i + 1) * P, :], in_=result[:])
 
-        with tc.psum_pool(name="psum_head", bufs=8) as psum:
-            nc.vector.memset(qT_words[:, L : L + 1], 0.0)
-            nc.vector.memset(eT_words[:, 0:1], 0.0)
-            transpose_pairs(nc, psum, ident_f32, e_raw, eT_words[:, 1 : L + 1], (False, False))
-            transpose_pairs(nc, psum, ident_f32, q_raw, qT_words[:, 0:L], (True, True))
-            store_z(psum, 0)
-            group_w()
-            store_z(psum, 1)
-            read_windows(0)
-            store_z(psum, 2)
-            read_windows(1)
-            quantise_w()
-            transpose_pairs(nc, psum, ident_f32, k_raw, kT[:].bitcast(F32), (True, True))
-            for b in range(L // X_KEYS):
-                transpose_x(psum, b)
-            for b in range(L // X_KEYS):
-                quantise_x(b)
-            store_z(psum, 3)
-            read_windows(2)
-            for g in range(KEY_PASSES):
-                project_values(psum, g)
+        Z_PIECES = ((0, 512), (512, 512), (1024, 128))
 
-        assert P * DV <= FIRST_SLOT
-        with ExitStack() as banks:
-            psum_zo = banks.enter_context(tc.psum_pool(name="psum_zo", bufs=4))
-            psum_s = banks.enter_context(tc.psum_pool(name="psum_s", bufs=2))
-            psum_e = banks.enter_context(tc.psum_pool(name="psum_e", bufs=2))
-            for n in range(TILES + 3):
-                if 0 <= n - 1 < TILES:
-                    exponentials(n - 1)
-                if n < TILES:
-                    scores(psum_s, n)
-                if n < KEY_PASSES:
-                    quantise_values(n)
-                if n + SLOTS + 1 < TILES:
-                    store_z(psum_zo, n + SLOTS + 1)
-                if n + SLOTS < TILES:
-                    read_windows(n + SLOTS)
-                if 0 <= n - 3 < TILES:
-                    multiply_e_v(psum_zo, n - 3)
-                if 0 <= n - 1 < TILES:
-                    transpose_e(psum_e, n - 1)
-                if 0 <= n - 2 < TILES:
-                    quantise_e(n - 2)
-                if 0 <= n - 3 < TILES:
-                    normalise_and_store(n - 3, n < TILES)
+        transpose_chunk("q", 0, S)
+        transpose_chunk("e", 0, V)
+        transpose_chunk("e", 256, S)
+        transpose_chunk("e", 512, V)
+        transpose_chunk("e", 768, S)
+        transpose_chunk("q", 256, V)
+        group_w()
+        z_piece(0, 0, 512, V)
+        z_piece(0, 512, 512, S)
+        z_piece(0, 1024, 128, V)
+        store_z(0)
+        z_piece(1, 0, 512, V)
+        z_piece(1, 512, 512, S)
+        z_piece(1, 1024, 128, S)
+        store_z(1)
+        transpose_x(0, V)
+        transpose_x(1, S)
+        quantise_w()
+        quantise_x(0)
+        z_piece(2, 0, 512, V)
+        z_piece(2, 512, 512, S)
+        z_piece(2, 1024, 128, S)
+        quantise_x(1)
+        read_windows(0)
+        store_z(2)
+        read_windows(1)
+        transpose_chunk("k", 0, S)
+        project_values(0, 0, V)
+        project_values(0, 1, S)
+        transpose_x(2, V)
+        project_values(0, 2, S)
+        transpose_x(3, V)
+        project_values(0, 3, S)
+        quantise_x(2)
+        quantise_x(3)
+        transpose_chunk("q", 512, S)
+        transpose_chunk("k", 512, V)
+        z_piece(3, 0, 512, V)
+        z_piece(3, 512, 512, S)
+        z_piece(3, 1024, 128, S)
+        store_z(3)
+        read_windows(2)
+        quantise_values(0)
+        multiply_qk(0, 0)
+        multiply_qk(0, 1)
+        for c in range(4):
+            project_values(1, c, S)
+
+        for n in range(TILES):
+            if n >= 1:
+                exponentials(n - 1)
+            add_scores(n, 0)
+            add_scores(n, 1)
+            if n >= LAG + 1:
+                normalise_and_store(n - LAG - 1, S)
+            if n >= LAG:
+                invert_row_sum(n - LAG)
+                quantise_e(n - LAG)
+            row_minimum(n)
+            if n == 0:
+                quantise_values(1)
+            if n + 1 < TILES:
+                multiply_qk(n + 1, 0)
+                multiply_qk(n + 1, 1)
+            if n + 4 < TILES:
+                for first, width in Z_PIECES:
+                    z_piece(n + 4, first, width, V if first == 0 else S)
+                store_z(n + 4)
+            if n + 3 < TILES:
+                read_windows(n + 3)
+            if n >= 1:
+                transpose_e(n - 1)
+                group_e(n - 1, S)
+            if n >= LAG:
+                multiply_e_v(n - LAG)
+        last = TILES - 1
+        for g in range(KEY_PASSES):
+            exponentials(last, g, g + 1)
+        for i in range(TILES - LAG, last):
+            invert_row_sum(i)
+            quantise_e(i)
+        normalise_and_store(4, V)
+        multiply_e_v(5)
+        transpose_e(last, 0, 1)
+        group_e(last, V, 0, 1)
+        multiply_e_v(6)
+        quantise_e(last, 0, 1)
+        normalise_and_store(5, S)
+        transpose_e(last, 1, 2)
+        group_e(last, V, 1, 2)
+        quantise_e(last, 1, 2)
+        normalise_and_store(6, S)
+        invert_row_sum(last)
+        multiply_e_v(last)
+        normalise_and_store(last, S, V)

@@ -58,7 +58,7 @@ def tile_relativeglobalattention_pa_kernel(tc, q, k, inputV, Wv, E, out):
         keep = ctx.enter_context(tc.tile_pool(name="keep", bufs=1))
         z_pool = ctx.enter_context(tc.tile_pool(name="z", bufs=5))
         s_pool = ctx.enter_context(tc.tile_pool(name="s", bufs=TILES))
-        work = ctx.enter_context(tc.tile_pool(name="work", bufs=5))
+        work = ctx.enter_context(tc.tile_pool(name="work", bufs=8))
         small = ctx.enter_context(tc.tile_pool(name="small", bufs=8))
         results = ctx.enter_context(tc.tile_pool(name="results", bufs=TILES + 1))
         psum = ctx.enter_context(tc.psum_pool(name="psum", bufs=8 - QK_BANKS))
@@ -313,13 +313,14 @@ def tile_relativeglobalattention_pa_kernel(tc, q, k, inputV, Wv, E, out):
                 e_keys_first[i, begin][:, : (end - begin) * 2 * P].rearrange("p (g u w) -> p g w u", u=2, w=P),
             )
 
+        def total_row_sum(i):
+            total = small.tile([P, 1], F32, name="total")
+            nc.vector.tensor_tensor(out=total[:], in0=row_sums[i][0][:], in1=row_sums[i][1][:], op=ALU.add)
+            row_sums[i] = [total]
+
         def invert_row_sum(i):
             inverse = small.tile([P, 1], F32, name="inverse")
-            total = row_sums[i][0]
-            if len(row_sums[i]) > 1:
-                total = small.tile([P, 1], F32, name="total")
-                nc.vector.tensor_tensor(out=total[:], in0=row_sums[i][0][:], in1=row_sums[i][1][:], op=ALU.add)
-            nc.vector.reciprocal(out=inverse[:], in_=total[:])
+            nc.vector.reciprocal(out=inverse[:], in_=row_sums[i][0][:])
             inverses[i] = inverse
 
         def quantise_e(i, begin=0, end=KEY_PASSES):
@@ -335,27 +336,32 @@ def tile_relativeglobalattention_pa_kernel(tc, q, k, inputV, Wv, E, out):
                 in_=e_grouped[i][:, begin * BANK : end * BANK],
             )
 
-        def multiply_e_v(i, begin=0, end=KEY_PASSES):
+        def multiply_e_v(i, parts=1):
             e_codes, e_scales = e_quantised[i]
-            if begin == 0:
-                sums[i] = psum.tile([P, DV], F32, name="bank")
-            for g in range(begin, end):
-                nc.tensor.matmul_mx(
-                    out=sums[i][:],
-                    lhsT=e_codes[:, g * P : (g + 1) * P].bitcast(FP8X4),
-                    lhsT_scale=e_scales[:, g * P : (g + 1) * P],
-                    rhs=v_codes[:, g * DV : (g + 1) * DV].bitcast(FP8X4),
-                    rhs_scale=v_scales[:, g * DV : (g + 1) * DV],
-                    start=(g == 0),
-                    stop=(g == KEY_PASSES - 1),
-                )
+            width = DV // parts
+            sums[i] = []
+            for part in range(parts):
+                acc = psum.tile([P, BANK], F32, name="bank")
+                for g in range(KEY_PASSES):
+                    cols = slice(g * DV + part * width, g * DV + (part + 1) * width)
+                    nc.tensor.matmul_mx(
+                        out=acc[:, :width],
+                        lhsT=e_codes[:, g * P : (g + 1) * P].bitcast(FP8X4),
+                        lhsT_scale=e_scales[:, g * P : (g + 1) * P],
+                        rhs=v_codes[:, cols].bitcast(FP8X4),
+                        rhs_scale=v_scales[:, cols],
+                        start=(g == 0),
+                        stop=(g == KEY_PASSES - 1),
+                    )
+                sums[i].append(acc)
 
         def normalise_and_store(i, *engines):
             result = results.tile([P, DV], F32, name="result")
             width = DV // len(engines)
-            for share, engine in enumerate(engines):
-                cols = slice(share * width, (share + 1) * width)
-                scaled_copy_out(nc, engine, result[:, cols], sums[i][:, cols], inverses[i][:])
+            for part, engine in enumerate(engines):
+                scaled_copy_out(
+                    nc, engine, result[:, part * width : (part + 1) * width], sums[i][part][:, :width], inverses[i][:]
+                )
             nc.sync.dma_start(out=out_rows[i * P : (i + 1) * P, :], in_=result[:])
 
         Z_PIECES = ((0, 512), (512, 512), (1024, 128))
@@ -402,7 +408,6 @@ def tile_relativeglobalattention_pa_kernel(tc, q, k, inputV, Wv, E, out):
         z_piece(3, 1024, 128, S)
         store_z(3)
         read_windows(2)
-        quantise_values(0)
         multiply_qk(0, 0)
         multiply_qk(0, 1)
         for c in range(4):
@@ -413,45 +418,52 @@ def tile_relativeglobalattention_pa_kernel(tc, q, k, inputV, Wv, E, out):
                 exponentials(n - 1)
             add_scores(n, 0)
             add_scores(n, 1)
+            if n >= 2:
+                group_e(n - 2, S)
             if n >= LAG + 1:
                 normalise_and_store(n - LAG - 1, S)
-            if n >= LAG:
+            if LAG <= n < TILES - 1:
                 invert_row_sum(n - LAG)
                 quantise_e(n - LAG)
             row_minimum(n)
-            if n == 0:
-                quantise_values(1)
+            if n < 2:
+                quantise_values(n)
             if n + 1 < TILES:
                 multiply_qk(n + 1, 0)
                 multiply_qk(n + 1, 1)
             if n + 4 < TILES:
                 for first, width in Z_PIECES:
-                    z_piece(n + 4, first, width, V if first == 0 else S)
+                    z_piece(n + 4, first, width, V if first == 1024 and n > 0 else S)
                 store_z(n + 4)
             if n + 3 < TILES:
                 read_windows(n + 3)
             if n >= 1:
                 transpose_e(n - 1)
-                group_e(n - 1, S)
-            if n >= LAG:
+            if LAG <= n < TILES - 1:
                 multiply_e_v(n - LAG)
         last = TILES - 1
-        for g in range(KEY_PASSES):
-            exponentials(last, g, g + 1)
-        for i in range(TILES - LAG, last):
-            invert_row_sum(i)
-            quantise_e(i)
-        normalise_and_store(4, V)
-        multiply_e_v(5)
+        exponentials(last, 0, 1)
+        exponentials(last, 1, 2)
+        invert_row_sum(4)
+        quantise_e(4)
+        multiply_e_v(4)
+        group_e(6, V)
+        invert_row_sum(5)
+        quantise_e(5)
         transpose_e(last, 0, 1)
         group_e(last, V, 0, 1)
-        multiply_e_v(6)
+        multiply_e_v(5)
+        invert_row_sum(6)
+        quantise_e(6)
+        total_row_sum(last)
         quantise_e(last, 0, 1)
-        normalise_and_store(5, S)
         transpose_e(last, 1, 2)
+        normalise_and_store(4, S)
+        invert_row_sum(last)
         group_e(last, V, 1, 2)
         quantise_e(last, 1, 2)
+        multiply_e_v(6)
+        normalise_and_store(5, S)
+        multiply_e_v(last, 2)
         normalise_and_store(6, S)
-        invert_row_sum(last)
-        multiply_e_v(last)
-        normalise_and_store(last, S, V)
+        normalise_and_store(last, V, S)

@@ -97,6 +97,14 @@ def tile_relativeglobalattention_pa_kernel(tc, q, k, inputV, Wv, E, out):
         load_x(1)
         load_chunk("q", q_rows, 512, 4)
 
+        zeros = const.tile([P, P], F32, name="zeros")
+        nc.vector.memset(zeros[:], 0.0)
+
+        def keep_clock(count):
+            bank = psum_qk.tile([P, BANK], F32, name="bank")
+            for step in range(count):
+                nc.tensor.matmul(out=bank[:, :P], lhsT=zeros[:], rhs=zeros[:], start=True, stop=True)
+
         ident_f32 = const.tile([P, P], F32, name="ident_f32")
         make_identity(nc, ident_f32[:])
 
@@ -366,6 +374,7 @@ def tile_relativeglobalattention_pa_kernel(tc, q, k, inputV, Wv, E, out):
 
         Z_PIECES = ((0, 512), (512, 512), (1024, 128))
 
+        keep_clock(4)
         transpose_chunk("q", 0, S)
         transpose_chunk("e", 0, V)
         transpose_chunk("e", 256, S)
@@ -373,6 +382,7 @@ def tile_relativeglobalattention_pa_kernel(tc, q, k, inputV, Wv, E, out):
         transpose_chunk("e", 768, S)
         transpose_chunk("q", 256, V)
         group_w()
+        keep_clock(2)
         z_piece(0, 0, 512, V)
         z_piece(0, 512, 512, S)
         z_piece(0, 1024, 128, V)
@@ -441,6 +451,10 @@ def tile_relativeglobalattention_pa_kernel(tc, q, k, inputV, Wv, E, out):
                 transpose_e(n - 1)
             if LAG <= n < TILES - 1:
                 multiply_e_v(n - LAG)
+            if n == 6:
+                keep_clock(2)
+            if n == 7:
+                keep_clock(2)
         last = TILES - 1
         exponentials(last, 0, 1)
         exponentials(last, 1, 2)

@@ -393,26 +393,26 @@ def tile_relativeglobalattention_pa_kernel(tc, q, k, inputV, Wv, E, out):
         store_z(1)
         transpose_x(0, V)
         transpose_x(1, S)
+        transpose_chunk("k", 0, S)
         quantise_w()
         quantise_x(0)
+        quantise_x(1)
         z_piece(2, 0, 512, V)
         z_piece(2, 512, 512, S)
         z_piece(2, 1024, 128, S)
-        quantise_x(1)
         read_windows(0)
         store_z(2)
         read_windows(1)
-        transpose_chunk("k", 0, S)
         project_values(0, 0, V)
         project_values(0, 1, S)
-        transpose_x(2, V)
-        project_values(0, 2, S)
-        transpose_x(3, V)
+        project_values(0, 2, V)
         project_values(0, 3, S)
+        transpose_x(2, V)
+        transpose_x(3, S)
+        transpose_chunk("q", 512, V)
+        transpose_chunk("k", 512, S)
         quantise_x(2)
         quantise_x(3)
-        transpose_chunk("q", 512, S)
-        transpose_chunk("k", 512, V)
         z_piece(3, 0, 512, V)
         z_piece(3, 512, 512, S)
         z_piece(3, 1024, 128, S)
@@ -432,12 +432,12 @@ def tile_relativeglobalattention_pa_kernel(tc, q, k, inputV, Wv, E, out):
                 group_e(n - 2, S)
             if n >= LAG + 1:
                 normalise_and_store(n - LAG - 1, S)
-            if LAG <= n < TILES - 1:
+            if n < 2:
+                quantise_values(n)
+            if n >= LAG:
                 invert_row_sum(n - LAG)
                 quantise_e(n - LAG)
             row_minimum(n)
-            if n < 2:
-                quantise_values(n)
             if n + 1 < TILES:
                 multiply_qk(n + 1, 0)
                 multiply_qk(n + 1, 1)
@@ -449,18 +449,13 @@ def tile_relativeglobalattention_pa_kernel(tc, q, k, inputV, Wv, E, out):
                 read_windows(n + 3)
             if n >= 1:
                 transpose_e(n - 1)
-            if LAG <= n < TILES - 1:
+            if n >= LAG:
                 multiply_e_v(n - LAG)
-            if n == 6:
-                keep_clock(2)
-            if n == 7:
+            if n >= TILES - 2:
                 keep_clock(2)
         last = TILES - 1
         exponentials(last, 0, 1)
         exponentials(last, 1, 2)
-        invert_row_sum(4)
-        quantise_e(4)
-        multiply_e_v(4)
         group_e(6, V)
         invert_row_sum(5)
         quantise_e(5)

@@ -22,9 +22,11 @@ KEY_PASSES = L // (P * PACK)
 X_KEYS = BANK // 2
 NEGATED_SCALE = -1.0 / 16.0
 
-Z_COLS = L + P
+Z_COLS = L + 1
+AREA = (P + 1) * Z_COLS + 15
 SLOTS = 3
-FIRST_SLOT = L * DV - SLOTS * P * Z_COLS
+FIRST_SLOT = L * DV - SLOTS * AREA
+Z_TILES = 5
 
 S, V = "scalar", "vector"
 QK_BANKS = 4
@@ -56,13 +58,15 @@ def tile_relativeglobalattention_pa_kernel(tc, q, k, inputV, Wv, E, out):
         ctx.enter_context(tc.manual_schedule())
         const = ctx.enter_context(tc.tile_pool(name="const", bufs=1))
         keep = ctx.enter_context(tc.tile_pool(name="keep", bufs=1))
-        z_pool = ctx.enter_context(tc.tile_pool(name="z", bufs=5))
         s_pool = ctx.enter_context(tc.tile_pool(name="s", bufs=TILES))
         work = ctx.enter_context(tc.tile_pool(name="work", bufs=8))
         small = ctx.enter_context(tc.tile_pool(name="small", bufs=8))
         results = ctx.enter_context(tc.tile_pool(name="results", bufs=TILES + 1))
         psum = ctx.enter_context(tc.psum_pool(name="psum", bufs=8 - QK_BANKS))
         psum_qk = ctx.enter_context(tc.psum_pool(name="psum_qk", bufs=QK_BANKS))
+
+        def tile_of(n):
+            return TILES - 1 - n
 
         def load_chunk(name, src, first, slots):
             chunk = keep.tile([P, slots * DK], BF16, name="%s_raw%d" % (name, first))
@@ -73,30 +77,33 @@ def tile_relativeglobalattention_pa_kernel(tc, q, k, inputV, Wv, E, out):
             raw[name, first] = (chunk, slots)
 
         raw = {}
-        load_chunk("q", q_rows, 0, 2)
+        load_chunk("q", q_rows, 768, 2)
         for quarter in range(4):
             load_chunk("e", E, 256 * quarter, 2)
-        load_chunk("q", q_rows, 256, 2)
-
         w_raw = keep.tile([P, PACK * DV], BF16, name="w_raw")
-        nc.sync.dma_start(
-            out=w_raw[:].rearrange("p (u x) -> p u x", u=2),
-            in_=Wv.rearrange("(u p h) c -> p u (h c)", u=2, h=2),
-        )
         x_raw = keep.tile([P, TILES * D], BF16, name="x_raw")
 
-        def load_x(half):
+        def load_w():
             nc.sync.dma_start(
-                out=x_raw[:].rearrange("p (s x) -> p s x", s=PACK)[:, 2 * half : 2 * half + 2, :],
-                in_=x_rows[half * BANK : (half + 1) * BANK, :].rearrange("(s p h) d -> p s (h d)", p=P, h=2),
+                out=w_raw[:].rearrange("p (u x) -> p u x", u=2),
+                in_=Wv.rearrange("(u p h) c -> p u (h c)", u=2, h=2),
             )
 
+        def load_x(b):
+            nc.sync.dma_start(
+                out=x_raw[:, 2 * b * D : 2 * (b + 1) * D],
+                in_=x_rows[b * X_KEYS : (b + 1) * X_KEYS, :].rearrange("(p h) d -> p (h d)", h=2),
+            )
+
+        load_chunk("q", q_rows, 512, 2)
+        load_w()
         load_x(0)
+        load_x(1)
         load_chunk("k", k_rows, 0, 4)
         load_chunk("k", k_rows, 512, 4)
-        load_x(1)
-        load_chunk("q", q_rows, 512, 4)
-
+        load_x(2)
+        load_x(3)
+        load_chunk("q", q_rows, 0, 4)
         zeros = const.tile([P, P], F32, name="zeros")
         nc.vector.memset(zeros[:], 0.0)
 
@@ -113,16 +120,14 @@ def tile_relativeglobalattention_pa_kernel(tc, q, k, inputV, Wv, E, out):
         nc.vector.memset(zero[:], 0.0)
         nc.scalar.activation(out=one[:], in_=zero[:], func=ACT.Exp)
 
-        E_FIRST = PACK
-        qT = keep.tile([P, 2 * (L + 1)], BF16, name="qT")
-        eT = keep.tile([P, 2 * (L + E_FIRST)], BF16, name="eT")
-        kT = keep.tile([P, 2 * L], BF16, name="kT")
-        transposed = {"q": (qT, 0), "e": (eT, E_FIRST), "k": (kT, 0)}
+        qT, eT, kT = (keep.tile([P, 2 * L], BF16, name="%sT" % label) for label in ("q", "e", "k"))
+        transposed = {"q": qT, "e": eT, "k": kT}
         qT_pairs = qT[:].rearrange("p (c h) -> p c h", h=2)
         eT_pairs = eT[:].rearrange("p (c h) -> p c h", h=2)
         kT_pairs = kT[:].rearrange("p (c h) -> p c h", h=2)
-        nc.vector.memset(qT[:].bitcast(F32)[:, L : L + 1], 0.0)
-        nc.vector.memset(eT[:].bitcast(F32)[:, 0:E_FIRST], 0.0)
+        z_buffers = [keep.tile([P, Z_COLS], F32, name="z%d" % index) for index in range(Z_TILES)]
+        for z in z_buffers:
+            nc.vector.memset(z[:, 0:1], 0.0)
 
         w_grouped = keep.tile([P, PACK * DV], BF16, name="w_grouped", align_bytes=64)
         w_codes = keep.tile([P, DV], U32, name="w_codes", align_bytes=64)
@@ -134,65 +139,58 @@ def tile_relativeglobalattention_pa_kernel(tc, q, k, inputV, Wv, E, out):
         v_codes = keep.tile([P, KEY_PASSES * DV], U32, name="v_codes", align_bytes=64)
         v_scales = keep.tile([P, KEY_PASSES * DV], U8, name="v_scales", align_bytes=64)
 
-        z_tiles, logits, qk, shifts, e_rows, row_sums, inverses, e_keys_first, e_grouped, e_quantised, sums = (
+        normalised, logits, qk, shifts, e_rows, row_sums, inverses, e_keys_first, e_grouped, e_quantised, sums = (
             {} for stage in range(11)
         )
 
         def transpose_chunk(name, first, engine):
-            dst, offset = transposed[name]
             chunk, slots = raw[name, first]
             words = chunk[:].bitcast(F32)
             bank = psum.tile([P, BANK], F32, name="bank")
             for t in range(slots):
                 nc.tensor.transpose(bank[:, t * P : (t + 1) * P], words[:, t * P : (t + 1) * P], ident_f32[:])
-            columns = slice(offset + first, offset + first + slots * P)
+            columns = slice(first, first + slots * P)
             copy_out(
                 nc,
                 engine,
-                dst[:].bitcast(F32)[:, columns].rearrange("p (r t) -> p r t", t=slots),
+                transposed[name][:].bitcast(F32)[:, columns].rearrange("p (r t) -> p r t", t=slots),
                 bank[:, : slots * P].rearrange("p (t r) -> p r t", t=slots),
             )
 
-        def z_piece(i, z_first, width, engine):
-            if i not in z_tiles:
-                z_tiles[i] = z_pool.tile([P, Z_COLS], F32, name="z")
-            first_part = (i + 1) * P
+        def z_piece(n, half, engine):
+            i = tile_of(n)
             bank = psum.tile([P, BANK], F32, name="bank")
-            spans = (
-                (0, z_first, min(z_first + width, first_part), E_FIRST + L - first_part),
-                (1, max(z_first, first_part), z_first + width, E_FIRST - 1 - first_part),
-            )
-            for next_query, begin, end, e_offset in spans:
-                if begin >= end:
-                    continue
-                queries = slice(i * P + next_query, (i + 1) * P + next_query)
-                for h in range(2):
-                    nc.tensor.matmul(
-                        out=bank[:, begin - z_first : end - z_first],
-                        lhsT=qT_pairs[:, queries, h],
-                        rhs=eT_pairs[:, e_offset + begin : e_offset + end, h],
-                        start=(h == 0),
-                        stop=(h == 1),
-                    )
-            scaled_copy_out(nc, engine, z_tiles[i][:, z_first : z_first + width], bank[:, :width], NEGATED_SCALE)
+            for h in range(2):
+                nc.tensor.matmul(
+                    out=bank[:],
+                    lhsT=qT_pairs[:, i * P : (i + 1) * P, h],
+                    rhs=eT_pairs[:, half * BANK : (half + 1) * BANK, h],
+                    start=(h == 0),
+                    stop=(h == 1),
+                )
+            first = 1 + half * BANK
+            scaled_copy_out(nc, engine, z_buffers[n % Z_TILES][:, first : first + BANK], bank[:], NEGATED_SCALE)
 
-        def store_z(i):
-            base = FIRST_SLOT + (i % SLOTS) * P * Z_COLS
+        def area(n):
+            first = FIRST_SLOT + n % SLOTS * AREA
+            return out_flat[first : first + AREA]
+
+        def store_z(n):
             nc.sync.dma_start(
-                out=out_flat[base : base + P * Z_COLS].rearrange("(p t) -> p t", t=Z_COLS),
-                in_=z_tiles[i][:],
+                out=area(n)[: P * Z_COLS].rearrange("(p t) -> p t", t=Z_COLS), in_=z_buffers[n % Z_TILES][:]
             )
+            width = L - (tile_of(n) + 1) * P
+            if width > 0:
+                nc.sync.dma_start(
+                    out=area(n)[P * Z_COLS : P * Z_COLS + width].rearrange("(p t) -> p t", p=1),
+                    in_=z_buffers[(n - 1) % Z_TILES][0:1, :width],
+                )
 
-        def read_windows(i):
-            base = FIRST_SLOT + (i % SLOTS) * P * Z_COLS
+        def read_windows(n):
+            first = L - tile_of(n) * P
             window = s_pool.tile([P, L], F32, name="window")
-            nc.sync.dma_start(
-                out=window[:],
-                in_=out_flat[base + P - 1 : base + P - 1 + P * (Z_COLS - 1)].rearrange(
-                    "(p t) -> p t", t=Z_COLS - 1
-                )[:, 0:L],
-            )
-            logits[i] = window
+            nc.sync.dma_start(out=window[:], in_=area(n)[first : first + P * L].rearrange("(p t) -> p t", t=L))
+            logits[n] = window
 
         def group_w():
             nc.gpsimd.tensor_scalar(
@@ -267,7 +265,7 @@ def tile_relativeglobalattention_pa_kernel(tc, q, k, inputV, Wv, E, out):
             for h in range(2):
                 nc.tensor.matmul(
                     out=bank[:],
-                    lhsT=qT_pairs[:, i * P : (i + 1) * P, h],
+                    lhsT=qT_pairs[:, tile_of(i) * P : (tile_of(i) + 1) * P, h],
                     rhs=kT_pairs[:, cols, h],
                     start=(h == 0),
                     stop=(h == 1),
@@ -363,33 +361,34 @@ def tile_relativeglobalattention_pa_kernel(tc, q, k, inputV, Wv, E, out):
                     )
                 sums[i].append(acc)
 
-        def normalise_and_store(i, *engines):
+        def normalise(i, *engines):
             result = results.tile([P, DV], F32, name="result")
             width = DV // len(engines)
             for part, engine in enumerate(engines):
                 scaled_copy_out(
                     nc, engine, result[:, part * width : (part + 1) * width], sums[i][part][:, :width], inverses[i][:]
                 )
-            nc.sync.dma_start(out=out_rows[i * P : (i + 1) * P, :], in_=result[:])
+            normalised[i] = result
 
-        Z_PIECES = ((0, 512), (512, 512), (1024, 128))
+        def store_result(i):
+            rows = slice(tile_of(i) * P, (tile_of(i) + 1) * P)
+            nc.sync.dma_start(out=out_rows[rows, :], in_=normalised[i][:])
+
 
         keep_clock(4)
-        transpose_chunk("q", 0, S)
+        transpose_chunk("q", 768, S)
         transpose_chunk("e", 0, V)
         transpose_chunk("e", 256, S)
         transpose_chunk("e", 512, V)
         transpose_chunk("e", 768, S)
-        transpose_chunk("q", 256, V)
         group_w()
         keep_clock(2)
-        z_piece(0, 0, 512, V)
-        z_piece(0, 512, 512, S)
-        z_piece(0, 1024, 128, V)
+        z_piece(0, 0, V)
+        z_piece(0, 1, S)
         store_z(0)
-        z_piece(1, 0, 512, V)
-        z_piece(1, 512, 512, S)
-        z_piece(1, 1024, 128, S)
+        transpose_chunk("q", 512, V)
+        z_piece(1, 0, V)
+        z_piece(1, 1, S)
         store_z(1)
         transpose_x(0, V)
         transpose_x(1, S)
@@ -397,9 +396,8 @@ def tile_relativeglobalattention_pa_kernel(tc, q, k, inputV, Wv, E, out):
         quantise_w()
         quantise_x(0)
         quantise_x(1)
-        z_piece(2, 0, 512, V)
-        z_piece(2, 512, 512, S)
-        z_piece(2, 1024, 128, S)
+        z_piece(2, 0, V)
+        z_piece(2, 1, S)
         read_windows(0)
         store_z(2)
         read_windows(1)
@@ -409,20 +407,20 @@ def tile_relativeglobalattention_pa_kernel(tc, q, k, inputV, Wv, E, out):
         project_values(0, 3, S)
         transpose_x(2, V)
         transpose_x(3, S)
-        transpose_chunk("q", 512, V)
         transpose_chunk("k", 512, S)
         quantise_x(2)
         quantise_x(3)
-        z_piece(3, 0, 512, V)
-        z_piece(3, 512, 512, S)
-        z_piece(3, 1024, 128, S)
+        transpose_chunk("q", 0, S)
+        z_piece(3, 0, V)
+        z_piece(3, 1, S)
         store_z(3)
         read_windows(2)
         multiply_qk(0, 0)
         multiply_qk(0, 1)
-        for c in range(4):
-            project_values(1, c, S)
-
+        project_values(1, 0, S)
+        project_values(1, 1, S)
+        project_values(1, 2, S)
+        project_values(1, 3, S)
         for n in range(TILES):
             if n >= 1:
                 exponentials(n - 1)
@@ -431,7 +429,7 @@ def tile_relativeglobalattention_pa_kernel(tc, q, k, inputV, Wv, E, out):
             if n >= 2:
                 group_e(n - 2, S)
             if n >= LAG + 1:
-                normalise_and_store(n - LAG - 1, S)
+                normalise(n - LAG - 1, S)
             if n < 2:
                 quantise_values(n)
             if n >= LAG:
@@ -442,11 +440,13 @@ def tile_relativeglobalattention_pa_kernel(tc, q, k, inputV, Wv, E, out):
                 multiply_qk(n + 1, 0)
                 multiply_qk(n + 1, 1)
             if n + 4 < TILES:
-                for first, width in Z_PIECES:
-                    z_piece(n + 4, first, width, V if first == 1024 and n > 0 else S)
+                z_piece(n + 4, 0, S)
+                z_piece(n + 4, 1, S)
                 store_z(n + 4)
             if n + 3 < TILES:
                 read_windows(n + 3)
+            if n >= LAG + 1:
+                store_result(n - LAG - 1)
             if n >= 1:
                 transpose_e(n - 1)
             if n >= LAG:
@@ -467,12 +467,16 @@ def tile_relativeglobalattention_pa_kernel(tc, q, k, inputV, Wv, E, out):
         total_row_sum(last)
         quantise_e(last, 0, 1)
         transpose_e(last, 1, 2)
-        normalise_and_store(4, S)
+        normalise(4, S)
+        store_result(4)
         invert_row_sum(last)
         group_e(last, V, 1, 2)
         quantise_e(last, 1, 2)
         multiply_e_v(6)
-        normalise_and_store(5, S)
+        normalise(5, S)
+        store_result(5)
         multiply_e_v(last, 2)
-        normalise_and_store(6, S)
-        normalise_and_store(last, V, S)
+        normalise(6, S)
+        store_result(6)
+        normalise(last, V, S)
+        store_result(last)

@@ -103,7 +103,6 @@ def tile_relativeglobalattention_pa_kernel(tc, q, k, inputV, Wv, E, out):
         load_chunk("k", k_rows, 512, 4)
         load_x(2)
         load_x(3)
-        load_chunk("q", q_rows, 0, 4)
         zeros = const.tile([P, P], F32, name="zeros")
         nc.vector.memset(zeros[:], 0.0)
 
@@ -186,11 +185,15 @@ def tile_relativeglobalattention_pa_kernel(tc, q, k, inputV, Wv, E, out):
                     in_=z_buffers[(n - 1) % Z_TILES][0:1, :width],
                 )
 
-        def read_windows(n):
+        def read_windows(n, begin=0, end=HALVES):
             first = L - tile_of(n) * P
-            window = s_pool.tile([P, L], F32, name="window")
-            nc.sync.dma_start(out=window[:], in_=area(n)[first : first + P * L].rearrange("(p t) -> p t", t=L))
-            logits[n] = window
+            if begin == 0:
+                logits[n] = s_pool.tile([P, L], F32, name="window")
+            cols = slice(begin * BANK, end * BANK)
+            nc.sync.dma_start(
+                out=logits[n][:, cols],
+                in_=area(n)[first : first + P * L].rearrange("(p t) -> p t", t=L)[:, cols],
+            )
 
         def group_w():
             nc.gpsimd.tensor_scalar(
@@ -279,9 +282,15 @@ def tile_relativeglobalattention_pa_kernel(tc, q, k, inputV, Wv, E, out):
                 out=t[:, cols], in0=qk[i, half][:], scalar=NEGATED_SCALE, in1=t[:, cols], op0=ALU.mult, op1=ALU.add
             )
 
-        def row_minimum(i):
-            shift = small.tile([P, 1], F32, name="shift")
-            nc.vector.tensor_reduce(out=shift[:], in_=logits[i][:], axis=AXIS.X, op=ALU.min)
+        def row_minimum(i, begin=0, end=HALVES):
+            shift = small.tile([P, 1], F32, name="shift%d" % begin)
+            nc.vector.tensor_reduce(
+                out=shift[:], in_=logits[i][:, begin * BANK : end * BANK], axis=AXIS.X, op=ALU.min
+            )
+            if begin > 0:
+                lesser = small.tile([P, 1], F32, name="lesser")
+                nc.vector.tensor_tensor(out=lesser[:], in0=shifts[i][:], in1=shift[:], op=ALU.min)
+                shift = lesser
             shifts[i] = shift
 
         def exponentials(i, begin=0, end=KEY_PASSES):
@@ -377,15 +386,16 @@ def tile_relativeglobalattention_pa_kernel(tc, q, k, inputV, Wv, E, out):
 
         keep_clock(4)
         transpose_chunk("q", 768, S)
+        keep_clock(1)
         transpose_chunk("e", 0, V)
         transpose_chunk("e", 256, S)
         transpose_chunk("e", 512, V)
         transpose_chunk("e", 768, S)
         group_w()
-        keep_clock(2)
         z_piece(0, 0, V)
         z_piece(0, 1, S)
         store_z(0)
+        load_chunk("q", q_rows, 0, 4)
         transpose_chunk("q", 512, V)
         z_piece(1, 0, V)
         z_piece(1, 1, S)
@@ -456,27 +466,27 @@ def tile_relativeglobalattention_pa_kernel(tc, q, k, inputV, Wv, E, out):
         last = TILES - 1
         exponentials(last, 0, 1)
         exponentials(last, 1, 2)
-        group_e(6, V)
         invert_row_sum(5)
         quantise_e(5)
-        transpose_e(last, 0, 1)
-        group_e(last, V, 0, 1)
         multiply_e_v(5)
+        group_e(6, V)
         invert_row_sum(6)
+        transpose_e(last, 0, 1)
         quantise_e(6)
-        total_row_sum(last)
-        quantise_e(last, 0, 1)
+        group_e(last, V, 0, 1)
         transpose_e(last, 1, 2)
+        total_row_sum(last)
+        group_e(last, V, 1, 2)
+        quantise_e(last, 0, 1)
+        invert_row_sum(last)
+        quantise_e(last, 1, 2)
         normalise(4, S)
         store_result(4)
-        invert_row_sum(last)
-        group_e(last, V, 1, 2)
-        quantise_e(last, 1, 2)
         multiply_e_v(6)
         normalise(5, S)
         store_result(5)
         multiply_e_v(last, 2)
-        normalise(6, S)
+        normalise(6, V)
         store_result(6)
-        normalise(last, V, S)
+        normalise(last, S, V)
         store_result(last)

@@ -29,7 +29,7 @@ FIRST_SLOT = L * DV - SLOTS * AREA
 Z_TILES = 5
 
 S, V = "scalar", "vector"
-QK_BANKS = 4
+QK_BANKS = 3
 LAG = 3
 
 FLOPS = 2 * L * (D * DV + 2 * L * DK + L * DV)
@@ -395,11 +395,11 @@ def tile_relativeglobalattention_pa_kernel(tc, q, k, inputV, Wv, E, out):
         z_piece(0, 0, V)
         z_piece(0, 1, S)
         store_z(0)
-        load_chunk("q", q_rows, 0, 4)
         transpose_chunk("q", 512, V)
         z_piece(1, 0, V)
         z_piece(1, 1, S)
         store_z(1)
+        load_chunk("q", q_rows, 0, 4)
         transpose_x(0, V)
         transpose_x(1, S)
         transpose_chunk("k", 0, S)
@@ -420,13 +420,13 @@ def tile_relativeglobalattention_pa_kernel(tc, q, k, inputV, Wv, E, out):
         transpose_chunk("k", 512, S)
         quantise_x(2)
         quantise_x(3)
-        transpose_chunk("q", 0, S)
         z_piece(3, 0, V)
         z_piece(3, 1, S)
         store_z(3)
         read_windows(2)
         multiply_qk(0, 0)
         multiply_qk(0, 1)
+        transpose_chunk("q", 0, S)
         project_values(1, 0, S)
         project_values(1, 1, S)
         project_values(1, 2, S)

@@ -78,8 +78,10 @@ def tile_relativeglobalattention_pa_kernel(tc, q, k, inputV, Wv, E, out):
 
         raw = {}
         load_chunk("q", q_rows, 768, 2)
-        for quarter in range(4):
-            load_chunk("e", E, 256 * quarter, 2)
+        load_chunk("e", E, 0, 2)
+        load_chunk("e", E, 256, 2)
+        load_chunk("e", E, 512, 2)
+        load_chunk("e", E, 768, 2)
         w_raw = keep.tile([P, PACK * DV], BF16, name="w_raw")
         x_raw = keep.tile([P, TILES * D], BF16, name="x_raw")
 
@@ -89,20 +91,18 @@ def tile_relativeglobalattention_pa_kernel(tc, q, k, inputV, Wv, E, out):
                 in_=Wv.rearrange("(u p h) c -> p u (h c)", u=2, h=2),
             )
 
-        def load_x(b):
+        def load_x(b, count):
             nc.sync.dma_start(
-                out=x_raw[:, 2 * b * D : 2 * (b + 1) * D],
-                in_=x_rows[b * X_KEYS : (b + 1) * X_KEYS, :].rearrange("(p h) d -> p (h d)", h=2),
+                out=x_raw[:].rearrange("p (b x) -> p b x", b=PACK)[:, b : b + count, :],
+                in_=x_rows[b * X_KEYS : (b + count) * X_KEYS, :].rearrange("(b p h) d -> p b (h d)", p=P, h=2),
             )
 
         load_chunk("q", q_rows, 512, 2)
         load_w()
-        load_x(0)
-        load_x(1)
+        load_x(0, 2)
         load_chunk("k", k_rows, 0, 4)
         load_chunk("k", k_rows, 512, 4)
-        load_x(2)
-        load_x(3)
+        load_x(2, 2)
         zeros = const.tile([P, P], F32, name="zeros")
         nc.vector.memset(zeros[:], 0.0)
 
@@ -142,18 +142,21 @@ def tile_relativeglobalattention_pa_kernel(tc, q, k, inputV, Wv, E, out):
             {} for stage in range(11)
         )
 
-        def transpose_chunk(name, first, engine):
+        def transpose_chunk(name, first, engine, part=0):
             chunk, slots = raw[name, first]
             words = chunk[:].bitcast(F32)
+            begin, end = 4 * part, min(4 * part + 4, slots)
             bank = psum.tile([P, BANK], F32, name="bank")
-            for t in range(slots):
-                nc.tensor.transpose(bank[:, t * P : (t + 1) * P], words[:, t * P : (t + 1) * P], ident_f32[:])
-            columns = slice(first, first + slots * P)
+            for t in range(begin, end):
+                nc.tensor.transpose(
+                    bank[:, (t - begin) * P : (t - begin + 1) * P], words[:, t * P : (t + 1) * P], ident_f32[:]
+                )
+            rows = transposed[name][:].bitcast(F32)[:, first : first + slots * P]
             copy_out(
                 nc,
                 engine,
-                transposed[name][:].bitcast(F32)[:, columns].rearrange("p (r t) -> p r t", t=slots),
-                bank[:, : slots * P].rearrange("p (t r) -> p r t", t=slots),
+                rows.rearrange("p (r t) -> p r t", t=slots)[:, :, begin:end],
+                bank[:, : (end - begin) * P].rearrange("p (t r) -> p r t", r=P),
             )
 
         def z_piece(n, half, engine):
@@ -425,9 +428,9 @@ def tile_relativeglobalattention_pa_kernel(tc, q, k, inputV, Wv, E, out):
         store_z(3)
         read_windows(2)
         multiply_qk(0, 0)
+        project_values(1, 0, V)
         multiply_qk(0, 1)
-        transpose_chunk("q", 0, S)
-        project_values(1, 0, S)
+        transpose_chunk("q", 0, V)
         project_values(1, 1, S)
         project_values(1, 2, S)
         project_values(1, 3, S)
@@ -436,6 +439,10 @@ def tile_relativeglobalattention_pa_kernel(tc, q, k, inputV, Wv, E, out):
                 exponentials(n - 1)
             add_scores(n, 0)
             add_scores(n, 1)
+            if n + 4 < TILES:
+                z_piece(n + 4, 0, S)
+                z_piece(n + 4, 1, S)
+                store_z(n + 4)
             if n >= 2:
                 group_e(n - 2, S)
             if n >= LAG + 1:
@@ -449,10 +456,6 @@ def tile_relativeglobalattention_pa_kernel(tc, q, k, inputV, Wv, E, out):
             if n + 1 < TILES:
                 multiply_qk(n + 1, 0)
                 multiply_qk(n + 1, 1)
-            if n + 4 < TILES:
-                z_piece(n + 4, 0, S)
-                z_piece(n + 4, 1, S)
-                store_z(n + 4)
             if n + 3 < TILES:
                 read_windows(n + 3)
             if n >= LAG + 1:

@@ -16,7 +16,7 @@ P = 128
 PACK = 4
 BANK = 512
 L, DK, D, DV = 1024, 256, 512, 512
-TILES = L // P
+STEPS = L // P
 HALVES = L // BANK
 KEY_PASSES = L // (P * PACK)
 X_KEYS = BANK // 2
@@ -24,29 +24,35 @@ NEGATED_SCALE = -1.0 / 16.0
 
 Z_COLS = L + 1
 AREA = (P + 1) * Z_COLS + 15
-SLOTS = 3
-FIRST_SLOT = L * DV - SLOTS * AREA
-Z_TILES = 5
+AREAS = 3
+FIRST_AREA = L * DV - AREAS * AREA
 
-S, V = "scalar", "vector"
+Z_AHEAD = 4
+E_LAG = 3
 QK_BANKS = 3
-LAG = 3
+
+SCALAR, VECTOR = "scalar", "vector"
 
 FLOPS = 2 * L * (D * DV + 2 * L * DK + L * DV)
 
 
 def copy_out(nc, engine, out, in_):
-    if engine == S:
+    if engine == SCALAR:
         nc.scalar.copy(out=out, in_=in_)
     else:
         nc.vector.tensor_copy(out=out, in_=in_)
 
 
 def scaled_copy_out(nc, engine, out, in_, factor):
-    if engine == S:
+    if engine == SCALAR:
         nc.scalar.activation(out=out, in_=in_, func=ACT.Copy, scale=factor)
     else:
         nc.vector.tensor_scalar_mul(out=out, in0=in_, scalar1=factor)
+
+
+def queries_of(n):
+    first = L - (n + 1) * P
+    return slice(first, first + P)
 
 
 def tile_relativeglobalattention_pa_kernel(tc, q, k, inputV, Wv, E, out):
@@ -58,57 +64,50 @@ def tile_relativeglobalattention_pa_kernel(tc, q, k, inputV, Wv, E, out):
         ctx.enter_context(tc.manual_schedule())
         const = ctx.enter_context(tc.tile_pool(name="const", bufs=1))
         keep = ctx.enter_context(tc.tile_pool(name="keep", bufs=1))
-        s_pool = ctx.enter_context(tc.tile_pool(name="s", bufs=TILES))
-        work = ctx.enter_context(tc.tile_pool(name="work", bufs=8))
-        small = ctx.enter_context(tc.tile_pool(name="small", bufs=8))
-        results = ctx.enter_context(tc.tile_pool(name="results", bufs=TILES + 1))
+        windows = ctx.enter_context(tc.tile_pool(name="windows", bufs=STEPS))
+        work = ctx.enter_context(tc.tile_pool(name="work", bufs=STEPS))
+        small = ctx.enter_context(tc.tile_pool(name="small", bufs=STEPS))
+        results = ctx.enter_context(tc.tile_pool(name="results", bufs=STEPS))
         psum = ctx.enter_context(tc.psum_pool(name="psum", bufs=8 - QK_BANKS))
         psum_qk = ctx.enter_context(tc.psum_pool(name="psum_qk", bufs=QK_BANKS))
 
-        def tile_of(n):
-            return TILES - 1 - n
+        raw = {}
 
         def load_chunk(name, src, first, slots):
             chunk = keep.tile([P, slots * DK], BF16, name="%s_raw%d" % (name, first))
             nc.sync.dma_start(
                 out=chunk[:],
-                in_=src[first : first + slots * P, :].rearrange("(p t) d -> p (t d)", t=slots),
+                in_=src[first : first + slots * P, :].rearrange("(r t) d -> r (t d)", t=slots),
             )
             raw[name, first] = (chunk, slots)
 
-        raw = {}
-        load_chunk("q", q_rows, 768, 2)
-        load_chunk("e", E, 0, 2)
-        load_chunk("e", E, 256, 2)
-        load_chunk("e", E, 512, 2)
-        load_chunk("e", E, 768, 2)
-        w_raw = keep.tile([P, PACK * DV], BF16, name="w_raw")
-        x_raw = keep.tile([P, TILES * D], BF16, name="x_raw")
-
-        def load_w():
-            nc.sync.dma_start(
-                out=w_raw[:].rearrange("p (u x) -> p u x", u=2),
-                in_=Wv.rearrange("(u p h) c -> p u (h c)", u=2, h=2),
-            )
-
         def load_x(b, count):
             nc.sync.dma_start(
-                out=x_raw[:].rearrange("p (b x) -> p b x", b=PACK)[:, b : b + count, :],
+                out=x_raw[:].rearrange("p (b x) -> p b x", b=L // X_KEYS)[:, b : b + count, :],
                 in_=x_rows[b * X_KEYS : (b + count) * X_KEYS, :].rearrange("(b p h) d -> p b (h d)", p=P, h=2),
             )
 
+        load_chunk("q", q_rows, 768, 2)
+        for first in range(0, L, 2 * P):
+            load_chunk("e", E, first, 2)
         load_chunk("q", q_rows, 512, 2)
-        load_w()
+        w_raw = keep.tile([P, PACK * DV], BF16, name="w_raw")
+        nc.sync.dma_start(
+            out=w_raw[:].rearrange("p (u x) -> p u x", u=2),
+            in_=Wv.rearrange("(u p h) c -> p u (h c)", u=2, h=2),
+        )
+        x_raw = keep.tile([P, STEPS * D], BF16, name="x_raw")
         load_x(0, 2)
         load_chunk("k", k_rows, 0, 4)
         load_chunk("k", k_rows, 512, 4)
         load_x(2, 2)
+
         zeros = const.tile([P, P], F32, name="zeros")
         nc.vector.memset(zeros[:], 0.0)
 
         def keep_clock(count):
             bank = psum_qk.tile([P, BANK], F32, name="bank")
-            for step in range(count):
+            for index in range(count):
                 nc.tensor.matmul(out=bank[:, :P], lhsT=zeros[:], rhs=zeros[:], start=True, stop=True)
 
         ident_f32 = const.tile([P, P], F32, name="ident_f32")
@@ -119,13 +118,12 @@ def tile_relativeglobalattention_pa_kernel(tc, q, k, inputV, Wv, E, out):
         nc.vector.memset(zero[:], 0.0)
         nc.scalar.activation(out=one[:], in_=zero[:], func=ACT.Exp)
 
-        qT, eT, kT = (keep.tile([P, 2 * L], BF16, name="%sT" % label) for label in ("q", "e", "k"))
+        qT, eT, kT = (keep.tile([P, 2 * L], BF16, name="%sT" % name) for name in ("q", "e", "k"))
         transposed = {"q": qT, "e": eT, "k": kT}
-        qT_pairs = qT[:].rearrange("p (c h) -> p c h", h=2)
-        eT_pairs = eT[:].rearrange("p (c h) -> p c h", h=2)
-        kT_pairs = kT[:].rearrange("p (c h) -> p c h", h=2)
-        z_buffers = [keep.tile([P, Z_COLS], F32, name="z%d" % index) for index in range(Z_TILES)]
-        for z in z_buffers:
+        qT_pairs, eT_pairs, kT_pairs = (a[:].rearrange("p (c h) -> p c h", h=2) for a in (qT, eT, kT))
+
+        z_tiles = [keep.tile([P, Z_COLS], F32, name="z%d" % index) for index in range(Z_AHEAD + 1)]
+        for z in z_tiles:
             nc.vector.memset(z[:, 0:1], 0.0)
 
         w_grouped = keep.tile([P, PACK * DV], BF16, name="w_grouped", align_bytes=64)
@@ -138,64 +136,58 @@ def tile_relativeglobalattention_pa_kernel(tc, q, k, inputV, Wv, E, out):
         v_codes = keep.tile([P, KEY_PASSES * DV], U32, name="v_codes", align_bytes=64)
         v_scales = keep.tile([P, KEY_PASSES * DV], U8, name="v_scales", align_bytes=64)
 
-        normalised, logits, qk, shifts, e_rows, row_sums, inverses, e_keys_first, e_grouped, e_quantised, sums = (
+        logits, qk, shifts, e_rows, row_sums, inverses, e_keys_first, e_grouped, e_quantised, sums, normalised = (
             {} for stage in range(11)
         )
 
-        def transpose_chunk(name, first, engine, part=0):
+        def transpose_chunk(name, first, engine):
             chunk, slots = raw[name, first]
             words = chunk[:].bitcast(F32)
-            begin, end = 4 * part, min(4 * part + 4, slots)
             bank = psum.tile([P, BANK], F32, name="bank")
-            for t in range(begin, end):
-                nc.tensor.transpose(
-                    bank[:, (t - begin) * P : (t - begin + 1) * P], words[:, t * P : (t + 1) * P], ident_f32[:]
-                )
-            rows = transposed[name][:].bitcast(F32)[:, first : first + slots * P]
+            for t in range(slots):
+                nc.tensor.transpose(bank[:, t * P : (t + 1) * P], words[:, t * P : (t + 1) * P], ident_f32[:])
             copy_out(
                 nc,
                 engine,
-                rows.rearrange("p (r t) -> p r t", t=slots)[:, :, begin:end],
-                bank[:, : (end - begin) * P].rearrange("p (t r) -> p r t", r=P),
+                transposed[name][:].bitcast(F32)[:, first : first + slots * P].rearrange("p (r t) -> p r t", t=slots),
+                bank[:, : slots * P].rearrange("p (t r) -> p r t", r=P),
             )
 
-        def z_piece(n, half, engine):
-            i = tile_of(n)
-            bank = psum.tile([P, BANK], F32, name="bank")
-            for h in range(2):
-                nc.tensor.matmul(
-                    out=bank[:],
-                    lhsT=qT_pairs[:, i * P : (i + 1) * P, h],
-                    rhs=eT_pairs[:, half * BANK : (half + 1) * BANK, h],
-                    start=(h == 0),
-                    stop=(h == 1),
-                )
-            first = 1 + half * BANK
-            scaled_copy_out(nc, engine, z_buffers[n % Z_TILES][:, first : first + BANK], bank[:], NEGATED_SCALE)
+        def compute_z(n, engines):
+            for half, engine in enumerate(engines):
+                cols = slice(half * BANK, (half + 1) * BANK)
+                bank = psum.tile([P, BANK], F32, name="bank")
+                for h in range(2):
+                    nc.tensor.matmul(
+                        out=bank[:],
+                        lhsT=qT_pairs[:, queries_of(n), h],
+                        rhs=eT_pairs[:, cols, h],
+                        start=(h == 0),
+                        stop=(h == 1),
+                    )
+                z = z_tiles[n % len(z_tiles)]
+                scaled_copy_out(nc, engine, z[:, 1 + cols.start : 1 + cols.stop], bank[:], NEGATED_SCALE)
 
         def area(n):
-            first = FIRST_SLOT + n % SLOTS * AREA
+            first = FIRST_AREA + n % AREAS * AREA
             return out_flat[first : first + AREA]
 
         def store_z(n):
             nc.sync.dma_start(
-                out=area(n)[: P * Z_COLS].rearrange("(p t) -> p t", t=Z_COLS), in_=z_buffers[n % Z_TILES][:]
+                out=area(n)[: P * Z_COLS].rearrange("(p t) -> p t", t=Z_COLS), in_=z_tiles[n % len(z_tiles)][:]
             )
-            width = L - (tile_of(n) + 1) * P
-            if width > 0:
+            reach = L - queries_of(n).stop
+            if reach > 0:
                 nc.sync.dma_start(
-                    out=area(n)[P * Z_COLS : P * Z_COLS + width].rearrange("(p t) -> p t", p=1),
-                    in_=z_buffers[(n - 1) % Z_TILES][0:1, :width],
+                    out=area(n)[P * Z_COLS : P * Z_COLS + reach].rearrange("(p t) -> p t", p=1),
+                    in_=z_tiles[(n - 1) % len(z_tiles)][0:1, :reach],
                 )
 
-        def read_windows(n, begin=0, end=HALVES):
-            first = L - tile_of(n) * P
-            if begin == 0:
-                logits[n] = s_pool.tile([P, L], F32, name="window")
-            cols = slice(begin * BANK, end * BANK)
+        def read_windows(n):
+            first = L - queries_of(n).start
+            logits[n] = windows.tile([P, L], F32, name="window")
             nc.sync.dma_start(
-                out=logits[n][:, cols],
-                in_=area(n)[first : first + P * L].rearrange("(p t) -> p t", t=L)[:, cols],
+                out=logits[n][:], in_=area(n)[first : first + P * L].rearrange("(p t) -> p t", t=L)
             )
 
         def group_w():
@@ -214,14 +206,11 @@ def tile_relativeglobalattention_pa_kernel(tc, q, k, inputV, Wv, E, out):
         def transpose_x(b, engine):
             x_words = x_raw[:].bitcast(F32)
             bank = psum.tile([P, BANK], F32, name="bank")
-            for s in range(X_KEYS // P):
-                t = b * (X_KEYS // P) + s
+            for h in range(2):
                 for u in range(2):
-                    nc.tensor.transpose(
-                        bank[:, u * X_KEYS + s * P : u * X_KEYS + (s + 1) * P],
-                        x_words[:, (2 * t + u) * P : (2 * t + u + 1) * P],
-                        ident_f32[:],
-                    )
+                    column = u * X_KEYS + h * P
+                    word = (2 * (2 * b + h) + u) * P
+                    nc.tensor.transpose(bank[:, column : column + P], x_words[:, word : word + P], ident_f32[:])
             copy_out(
                 nc,
                 engine,
@@ -234,7 +223,7 @@ def tile_relativeglobalattention_pa_kernel(tc, q, k, inputV, Wv, E, out):
             nc.vector.quantize_mx(
                 out=x_codes[:, keys].bitcast(FP8X4),
                 scales=x_scales[:, keys],
-                in_=x_grouped[:, b * X_KEYS * PACK : (b + 1) * X_KEYS * PACK],
+                in_=x_grouped[:, keys.start * PACK : keys.stop * PACK],
             )
 
         def project_values(g, c, engine):
@@ -265,105 +254,96 @@ def tile_relativeglobalattention_pa_kernel(tc, q, k, inputV, Wv, E, out):
                 in_=v_grouped[:, g * DV * PACK : (g + 1) * DV * PACK],
             )
 
-        def multiply_qk(i, half):
-            cols = slice(half * BANK, (half + 1) * BANK)
+        def multiply_qk(n, half):
             bank = psum_qk.tile([P, BANK], F32, name="bank")
             for h in range(2):
                 nc.tensor.matmul(
                     out=bank[:],
-                    lhsT=qT_pairs[:, tile_of(i) * P : (tile_of(i) + 1) * P, h],
-                    rhs=kT_pairs[:, cols, h],
+                    lhsT=qT_pairs[:, queries_of(n), h],
+                    rhs=kT_pairs[:, half * BANK : (half + 1) * BANK, h],
                     start=(h == 0),
                     stop=(h == 1),
                 )
-            qk[i, half] = bank
+            qk[n, half] = bank
 
-        def add_scores(i, half):
-            cols = slice(half * BANK, (half + 1) * BANK)
-            t = logits[i]
+        def add_scores(n, half):
+            t = logits[n][:, half * BANK : (half + 1) * BANK]
             nc.vector.scalar_tensor_tensor(
-                out=t[:, cols], in0=qk[i, half][:], scalar=NEGATED_SCALE, in1=t[:, cols], op0=ALU.mult, op1=ALU.add
+                out=t, in0=qk[n, half][:], scalar=NEGATED_SCALE, in1=t, op0=ALU.mult, op1=ALU.add
             )
 
-        def row_minimum(i, begin=0, end=HALVES):
-            shift = small.tile([P, 1], F32, name="shift%d" % begin)
-            nc.vector.tensor_reduce(
-                out=shift[:], in_=logits[i][:, begin * BANK : end * BANK], axis=AXIS.X, op=ALU.min
-            )
-            if begin > 0:
-                lesser = small.tile([P, 1], F32, name="lesser")
-                nc.vector.tensor_tensor(out=lesser[:], in0=shifts[i][:], in1=shift[:], op=ALU.min)
-                shift = lesser
-            shifts[i] = shift
+        def row_minimum(n):
+            shifts[n] = small.tile([P, 1], F32, name="shift")
+            nc.vector.tensor_reduce(out=shifts[n][:], in_=logits[n][:], axis=AXIS.X, op=ALU.min)
 
-        def exponentials(i, begin=0, end=KEY_PASSES):
+
+        def exponentials(n, begin=0, end=KEY_PASSES):
             if begin == 0:
-                e_rows[i] = work.tile([P, L], BF16, name="e_bf16")
-                row_sums[i] = []
+                e_rows[n] = work.tile([P, L], BF16, name="e_bf16")
+                row_sums[n] = []
             row_sum = small.tile([P, 1], F32, name="row_sum%d" % begin)
-            cols = slice(begin * BANK, end * BANK)
+            keys = slice(begin * BANK, end * BANK)
             nc.scalar.activation(
-                out=e_rows[i][:, cols],
-                in_=logits[i][:, cols],
+                out=e_rows[n][:, keys],
+                in_=logits[n][:, keys],
                 func=ACT.Exp,
-                bias=shifts[i][:],
+                bias=shifts[n][:],
                 scale=-1.0,
                 accum_out=row_sum[:],
             )
-            row_sums[i].append(row_sum)
+            row_sums[n].append(row_sum)
 
-        def transpose_e(i, begin=0, end=KEY_PASSES):
-            e_words = e_rows[i][:].bitcast(F32)
+        def transpose_e(n, begin=0, end=KEY_PASSES):
+            e_words = e_rows[n][:].bitcast(F32)
             bank = psum.tile([P, BANK], F32, name="bank")
-            for s in range(2 * begin, 2 * end):
+            for column, word in enumerate(range(2 * begin, 2 * end)):
                 nc.tensor.transpose(
-                    bank[:, (s - 2 * begin) * P : (s - 2 * begin + 1) * P], e_words[:, s * P : (s + 1) * P], ident_f32[:]
+                    bank[:, column * P : (column + 1) * P], e_words[:, word * P : (word + 1) * P], ident_f32[:]
                 )
-            e_keys_first[i, begin] = bank
+            e_keys_first[n, begin] = bank
 
-        def group_e(i, engine, begin=0, end=KEY_PASSES):
+        def group_e(n, engine, begin=0, end=KEY_PASSES):
             if begin == 0:
-                e_grouped[i] = work.tile([P, L], BF16, name="e_grouped", align_bytes=64)
+                e_grouped[n] = work.tile([P, L], BF16, name="e_grouped", align_bytes=64)
             copy_out(
                 nc,
                 engine,
-                e_grouped[i][:].bitcast(F32).rearrange("p (g w u) -> p g w u", g=KEY_PASSES, u=2)[:, begin:end],
-                e_keys_first[i, begin][:, : (end - begin) * 2 * P].rearrange("p (g u w) -> p g w u", u=2, w=P),
+                e_grouped[n][:].bitcast(F32).rearrange("p (g w u) -> p g w u", g=KEY_PASSES, u=2)[:, begin:end],
+                e_keys_first[n, begin][:, : (end - begin) * 2 * P].rearrange("p (g u w) -> p g w u", u=2, w=P),
             )
 
-        def total_row_sum(i):
-            total = small.tile([P, 1], F32, name="total")
-            nc.vector.tensor_tensor(out=total[:], in0=row_sums[i][0][:], in1=row_sums[i][1][:], op=ALU.add)
-            row_sums[i] = [total]
-
-        def invert_row_sum(i):
-            inverse = small.tile([P, 1], F32, name="inverse")
-            nc.vector.reciprocal(out=inverse[:], in_=row_sums[i][0][:])
-            inverses[i] = inverse
-
-        def quantise_e(i, begin=0, end=KEY_PASSES):
+        def quantise_e(n, begin=0, end=KEY_PASSES):
             if begin == 0:
                 e_codes = work.tile([P, KEY_PASSES * P], U32, name="e_codes", align_bytes=64)
                 e_scales = work.tile([P, KEY_PASSES * P], U8, name="e_scales", align_bytes=64)
-                e_quantised[i] = (e_codes, e_scales)
-            e_codes, e_scales = e_quantised[i]
+                e_quantised[n] = (e_codes, e_scales)
+            e_codes, e_scales = e_quantised[n]
             words = slice(begin * P, end * P)
             nc.vector.quantize_mx(
                 out=e_codes[:, words].bitcast(FP8X4),
                 scales=e_scales[:, words],
-                in_=e_grouped[i][:, begin * BANK : end * BANK],
+                in_=e_grouped[n][:, begin * BANK : end * BANK],
             )
 
-        def multiply_e_v(i, parts=1):
-            e_codes, e_scales = e_quantised[i]
+        def total_row_sum(n):
+            total = small.tile([P, 1], F32, name="total")
+            nc.vector.tensor_tensor(out=total[:], in0=row_sums[n][0][:], in1=row_sums[n][1][:], op=ALU.add)
+            row_sums[n] = [total]
+
+        def invert_row_sum(n):
+            inverses[n] = small.tile([P, 1], F32, name="inverse")
+            nc.vector.reciprocal(out=inverses[n][:], in_=row_sums[n][0][:])
+
+        def multiply_e_v(n, parts=1):
+            e_codes, e_scales = e_quantised[n]
             width = DV // parts
-            sums[i] = []
+            sums[n] = []
             for part in range(parts):
-                acc = psum.tile([P, BANK], F32, name="bank")
+                bank = psum.tile([P, BANK], F32, name="bank")
                 for g in range(KEY_PASSES):
                     cols = slice(g * DV + part * width, g * DV + (part + 1) * width)
                     nc.tensor.matmul_mx(
-                        out=acc[:, :width],
+                        out=bank[:, :width],
                         lhsT=e_codes[:, g * P : (g + 1) * P].bitcast(FP8X4),
                         lhsT_scale=e_scales[:, g * P : (g + 1) * P],
                         rhs=v_codes[:, cols].bitcast(FP8X4),
@@ -371,125 +351,116 @@ def tile_relativeglobalattention_pa_kernel(tc, q, k, inputV, Wv, E, out):
                         start=(g == 0),
                         stop=(g == KEY_PASSES - 1),
                     )
-                sums[i].append(acc)
+                sums[n].append(bank)
 
-        def normalise(i, *engines):
-            result = results.tile([P, DV], F32, name="result")
+        def normalise(n, *engines):
+            normalised[n] = results.tile([P, DV], F32, name="result")
             width = DV // len(engines)
             for part, engine in enumerate(engines):
-                scaled_copy_out(
-                    nc, engine, result[:, part * width : (part + 1) * width], sums[i][part][:, :width], inverses[i][:]
-                )
-            normalised[i] = result
+                cols = slice(part * width, (part + 1) * width)
+                scaled_copy_out(nc, engine, normalised[n][:, cols], sums[n][part][:, :width], inverses[n][:])
 
-        def store_result(i):
-            rows = slice(tile_of(i) * P, (tile_of(i) + 1) * P)
-            nc.sync.dma_start(out=out_rows[rows, :], in_=normalised[i][:])
+        def store_result(n):
+            nc.sync.dma_start(out=out_rows[queries_of(n), :], in_=normalised[n][:])
 
-
+        turns = (VECTOR, SCALAR, VECTOR, SCALAR)
         keep_clock(4)
-        transpose_chunk("q", 768, S)
+        transpose_chunk("q", 768, SCALAR)
         keep_clock(1)
-        transpose_chunk("e", 0, V)
-        transpose_chunk("e", 256, S)
-        transpose_chunk("e", 512, V)
-        transpose_chunk("e", 768, S)
+        for index, engine in enumerate(turns):
+            transpose_chunk("e", 2 * P * index, engine)
         group_w()
-        z_piece(0, 0, V)
-        z_piece(0, 1, S)
+        compute_z(0, (VECTOR, SCALAR))
         store_z(0)
-        transpose_chunk("q", 512, V)
-        z_piece(1, 0, V)
-        z_piece(1, 1, S)
+        transpose_chunk("q", 512, VECTOR)
+        compute_z(1, (VECTOR, SCALAR))
         store_z(1)
         load_chunk("q", q_rows, 0, 4)
-        transpose_x(0, V)
-        transpose_x(1, S)
-        transpose_chunk("k", 0, S)
+        transpose_x(0, VECTOR)
+        transpose_x(1, SCALAR)
+        transpose_chunk("k", 0, SCALAR)
         quantise_w()
         quantise_x(0)
         quantise_x(1)
-        z_piece(2, 0, V)
-        z_piece(2, 1, S)
+        compute_z(2, (VECTOR, SCALAR))
         read_windows(0)
         store_z(2)
         read_windows(1)
-        project_values(0, 0, V)
-        project_values(0, 1, S)
-        project_values(0, 2, V)
-        project_values(0, 3, S)
-        transpose_x(2, V)
-        transpose_x(3, S)
-        transpose_chunk("k", 512, S)
+        for c, engine in enumerate(turns):
+            project_values(0, c, engine)
+        transpose_x(2, VECTOR)
+        transpose_x(3, SCALAR)
+        transpose_chunk("k", 512, SCALAR)
         quantise_x(2)
         quantise_x(3)
-        z_piece(3, 0, V)
-        z_piece(3, 1, S)
+        compute_z(3, (VECTOR, SCALAR))
         store_z(3)
         read_windows(2)
+        transpose_chunk("q", 0, SCALAR)
         multiply_qk(0, 0)
-        project_values(1, 0, V)
+        project_values(1, 0, VECTOR)
         multiply_qk(0, 1)
-        transpose_chunk("q", 0, V)
-        project_values(1, 1, S)
-        project_values(1, 2, S)
-        project_values(1, 3, S)
-        for n in range(TILES):
+        project_values(1, 1, SCALAR)
+        project_values(1, 2, SCALAR)
+
+        for n in range(STEPS):
             if n >= 1:
                 exponentials(n - 1)
             add_scores(n, 0)
             add_scores(n, 1)
-            if n + 4 < TILES:
-                z_piece(n + 4, 0, S)
-                z_piece(n + 4, 1, S)
-                store_z(n + 4)
+            if n + Z_AHEAD < STEPS:
+                compute_z(n + Z_AHEAD, (SCALAR, SCALAR))
+                store_z(n + Z_AHEAD)
+            if n == 0:
+                project_values(1, 3, SCALAR)
             if n >= 2:
-                group_e(n - 2, S)
-            if n >= LAG + 1:
-                normalise(n - LAG - 1, S)
-            if n < 2:
+                group_e(n - 2, SCALAR)
+            if n >= E_LAG + 1:
+                normalise(n - E_LAG - 1, SCALAR)
+            if n < KEY_PASSES:
                 quantise_values(n)
-            if n >= LAG:
-                invert_row_sum(n - LAG)
-                quantise_e(n - LAG)
+            if n >= E_LAG:
+                invert_row_sum(n - E_LAG)
+                quantise_e(n - E_LAG)
             row_minimum(n)
-            if n + 1 < TILES:
+            if n + 1 < STEPS:
                 multiply_qk(n + 1, 0)
                 multiply_qk(n + 1, 1)
-            if n + 3 < TILES:
-                read_windows(n + 3)
-            if n >= LAG + 1:
-                store_result(n - LAG - 1)
+            if n + Z_AHEAD - 1 < STEPS:
+                read_windows(n + Z_AHEAD - 1)
+            if n >= E_LAG + 1:
+                store_result(n - E_LAG - 1)
             if n >= 1:
                 transpose_e(n - 1)
-            if n >= LAG:
-                multiply_e_v(n - LAG)
-            if n >= TILES - 2:
+            if n >= E_LAG:
+                multiply_e_v(n - E_LAG)
+            if n >= STEPS - 2:
                 keep_clock(2)
-        last = TILES - 1
-        exponentials(last, 0, 1)
-        exponentials(last, 1, 2)
-        invert_row_sum(5)
-        quantise_e(5)
-        multiply_e_v(5)
-        group_e(6, V)
-        invert_row_sum(6)
+
+        last = STEPS - 1
+        for g in range(KEY_PASSES):
+            exponentials(last, g, g + 1)
+        invert_row_sum(last - 2)
+        quantise_e(last - 2)
+        multiply_e_v(last - 2)
+        group_e(last - 1, VECTOR)
+        invert_row_sum(last - 1)
         transpose_e(last, 0, 1)
-        quantise_e(6)
-        group_e(last, V, 0, 1)
+        quantise_e(last - 1)
+        group_e(last, VECTOR, 0, 1)
         transpose_e(last, 1, 2)
         total_row_sum(last)
-        group_e(last, V, 1, 2)
+        group_e(last, VECTOR, 1, 2)
         quantise_e(last, 0, 1)
         invert_row_sum(last)
         quantise_e(last, 1, 2)
-        normalise(4, S)
-        store_result(4)
-        multiply_e_v(6)
-        normalise(5, S)
-        store_result(5)
+        normalise(last - 3, SCALAR)
+        store_result(last - 3)
+        multiply_e_v(last - 1)
+        normalise(last - 2, SCALAR)
+        store_result(last - 2)
         multiply_e_v(last, 2)
-        normalise(6, V)
-        store_result(6)
-        normalise(last, S, V)
+        normalise(last - 1, VECTOR)
+        store_result(last - 1)
+        normalise(last, SCALAR, VECTOR)
         store_result(last)

from contextlib import ExitStack

import concourse.mybir as mybir
from concourse.masks import make_identity

F32 = mybir.dt.float32
BF16 = mybir.dt.bfloat16
U32 = mybir.dt.uint32
U8 = mybir.dt.uint8
FP8X4 = mybir.dt.float8_e4m3fn_x4
ACT = mybir.ActivationFunctionType
ALU = mybir.AluOpType
AXIS = mybir.AxisListType

P = 128
PACK = 4
BANK = 512
L, DK, D, DV = 1024, 256, 512, 512
STEPS = L // P
HALVES = L // BANK
KEY_PASSES = L // (P * PACK)
X_KEYS = BANK // 2
NEGATED_SCALE = -1.0 / 16.0

Z_COLS = L + 1
AREA = (P + 1) * Z_COLS + 15
AREAS = 3
FIRST_AREA = L * DV - AREAS * AREA

Z_AHEAD = 4
E_LAG = 3
QK_BANKS = 3

SCALAR, VECTOR = "scalar", "vector"

FLOPS = 2 * L * (D * DV + 2 * L * DK + L * DV)


def copy_out(nc, engine, out, in_):
    if engine == SCALAR:
        nc.scalar.copy(out=out, in_=in_)
    else:
        nc.vector.tensor_copy(out=out, in_=in_)


def scaled_copy_out(nc, engine, out, in_, factor):
    if engine == SCALAR:
        nc.scalar.activation(out=out, in_=in_, func=ACT.Copy, scale=factor)
    else:
        nc.vector.tensor_scalar_mul(out=out, in0=in_, scalar1=factor)


def queries_of(n):
    first = L - (n + 1) * P
    return slice(first, first + P)


def tile_relativeglobalattention_pa_kernel(tc, q, k, inputV, Wv, E, out):
    nc = tc.nc
    q_rows, k_rows, x_rows, out_rows = (a.flatten_outer_dims() for a in (q, k, inputV, out))
    out_flat = out.rearrange("b l d -> (b l d)")

    with ExitStack() as ctx:
        ctx.enter_context(tc.manual_schedule())
        const = ctx.enter_context(tc.tile_pool(name="const", bufs=1))
        keep = ctx.enter_context(tc.tile_pool(name="keep", bufs=1))
        windows = ctx.enter_context(tc.tile_pool(name="windows", bufs=STEPS))
        work = ctx.enter_context(tc.tile_pool(name="work", bufs=STEPS))
        small = ctx.enter_context(tc.tile_pool(name="small", bufs=STEPS))
        results = ctx.enter_context(tc.tile_pool(name="results", bufs=STEPS))
        psum = ctx.enter_context(tc.psum_pool(name="psum", bufs=8 - QK_BANKS))
        psum_qk = ctx.enter_context(tc.psum_pool(name="psum_qk", bufs=QK_BANKS))

        raw = {}

        def load_chunk(name, src, first, slots):
            chunk = keep.tile([P, slots * DK], BF16, name="%s_raw%d" % (name, first))
            nc.sync.dma_start(
                out=chunk[:],
                in_=src[first : first + slots * P, :].rearrange("(r t) d -> r (t d)", t=slots),
            )
            raw[name, first] = (chunk, slots)

        def load_x(b, count):
            nc.sync.dma_start(
                out=x_raw[:].rearrange("p (b x) -> p b x", b=L // X_KEYS)[:, b : b + count, :],
                in_=x_rows[b * X_KEYS : (b + count) * X_KEYS, :].rearrange("(b p h) d -> p b (h d)", p=P, h=2),
            )

        load_chunk("q", q_rows, 768, 2)
        for first in range(0, L, 2 * P):
            load_chunk("e", E, first, 2)
        load_chunk("q", q_rows, 512, 2)
        w_raw = keep.tile([P, PACK * DV], BF16, name="w_raw")
        nc.sync.dma_start(
            out=w_raw[:].rearrange("p (u x) -> p u x", u=2),
            in_=Wv.rearrange("(u p h) c -> p u (h c)", u=2, h=2),
        )
        x_raw = keep.tile([P, STEPS * D], BF16, name="x_raw")
        load_x(0, 2)
        load_chunk("k", k_rows, 0, 4)
        load_chunk("k", k_rows, 512, 4)
        load_x(2, 2)

        zeros = const.tile([P, P], F32, name="zeros")
        nc.vector.memset(zeros[:], 0.0)

        def keep_clock(count):
            bank = psum_qk.tile([P, BANK], F32, name="bank")
            for index in range(count):
                nc.tensor.matmul(out=bank[:, :P], lhsT=zeros[:], rhs=zeros[:], start=True, stop=True)

        ident_f32 = const.tile([P, P], F32, name="ident_f32")
        make_identity(nc, ident_f32[:])

        zero = const.tile([P, 1], F32, name="zero")
        one = const.tile([P, 1], F32, name="one")
        nc.vector.memset(zero[:], 0.0)
        nc.scalar.activation(out=one[:], in_=zero[:], func=ACT.Exp)

        qT, eT, kT = (keep.tile([P, 2 * L], BF16, name="%sT" % name) for name in ("q", "e", "k"))
        transposed = {"q": qT, "e": eT, "k": kT}
        qT_pairs, eT_pairs, kT_pairs = (a[:].rearrange("p (c h) -> p c h", h=2) for a in (qT, eT, kT))

        z_tiles = [keep.tile([P, Z_COLS], F32, name="z%d" % index) for index in range(Z_AHEAD + 1)]
        for z in z_tiles:
            nc.vector.memset(z[:, 0:1], 0.0)

        w_grouped = keep.tile([P, PACK * DV], BF16, name="w_grouped", align_bytes=64)
        w_codes = keep.tile([P, DV], U32, name="w_codes", align_bytes=64)
        w_scales = keep.tile([P, DV], U8, name="w_scales", align_bytes=64)
        x_grouped = keep.tile([P, PACK * L], BF16, name="x_grouped", align_bytes=64)
        x_codes = keep.tile([P, L], U32, name="x_codes", align_bytes=64)
        x_scales = keep.tile([P, L], U8, name="x_scales", align_bytes=64)
        v_grouped = keep.tile([P, KEY_PASSES * PACK * DV], BF16, name="v_grouped", align_bytes=64)
        v_codes = keep.tile([P, KEY_PASSES * DV], U32, name="v_codes", align_bytes=64)
        v_scales = keep.tile([P, KEY_PASSES * DV], U8, name="v_scales", align_bytes=64)

        logits, qk, shifts, e_rows, row_sums, inverses, e_keys_first, e_grouped, e_quantised, sums, normalised = (
            {} for stage in range(11)
        )

        def transpose_chunk(name, first, engine):
            chunk, slots = raw[name, first]
            words = chunk[:].bitcast(F32)
            bank = psum.tile([P, BANK], F32, name="bank")
            for t in range(slots):
                nc.tensor.transpose(bank[:, t * P : (t + 1) * P], words[:, t * P : (t + 1) * P], ident_f32[:])
            copy_out(
                nc,
                engine,
                transposed[name][:].bitcast(F32)[:, first : first + slots * P].rearrange("p (r t) -> p r t", t=slots),
                bank[:, : slots * P].rearrange("p (t r) -> p r t", r=P),
            )

        def compute_z(n, engines):
            for half, engine in enumerate(engines):
                cols = slice(half * BANK, (half + 1) * BANK)
                bank = psum.tile([P, BANK], F32, name="bank")
                for h in range(2):
                    nc.tensor.matmul(
                        out=bank[:],
                        lhsT=qT_pairs[:, queries_of(n), h],
                        rhs=eT_pairs[:, cols, h],
                        start=(h == 0),
                        stop=(h == 1),
                    )
                z = z_tiles[n % len(z_tiles)]
                scaled_copy_out(nc, engine, z[:, 1 + cols.start : 1 + cols.stop], bank[:], NEGATED_SCALE)

        def area(n):
            first = FIRST_AREA + n % AREAS * AREA
            return out_flat[first : first + AREA]

        def store_z(n):
            nc.sync.dma_start(
                out=area(n)[: P * Z_COLS].rearrange("(p t) -> p t", t=Z_COLS), in_=z_tiles[n % len(z_tiles)][:]
            )
            reach = L - queries_of(n).stop
            if reach > 0:
                nc.sync.dma_start(
                    out=area(n)[P * Z_COLS : P * Z_COLS + reach].rearrange("(p t) -> p t", p=1),
                    in_=z_tiles[(n - 1) % len(z_tiles)][0:1, :reach],
                )

        def read_windows(n):
            first = L - queries_of(n).start
            logits[n] = windows.tile([P, L], F32, name="window")
            nc.sync.dma_start(
                out=logits[n][:], in_=area(n)[first : first + P * L].rearrange("(p t) -> p t", t=L)
            )

        def group_w():
            nc.gpsimd.tensor_scalar(
                out=w_grouped[:].rearrange("p (c t) -> p c t", t=PACK),
                in0=w_raw[:].rearrange("p (t c) -> p c t", t=PACK),
                scalar1=1.0,
                scalar2=0.0,
                op0=ALU.mult,
                op1=ALU.add,
            )

        def quantise_w():
            nc.vector.quantize_mx(out=w_codes[:].bitcast(FP8X4), scales=w_scales[:], in_=w_grouped[:])

        def transpose_x(b, engine):
            x_words = x_raw[:].bitcast(F32)
            bank = psum.tile([P, BANK], F32, name="bank")
            for h in range(2):
                for u in range(2):
                    column = u * X_KEYS + h * P
                    word = (2 * (2 * b + h) + u) * P
                    nc.tensor.transpose(bank[:, column : column + P], x_words[:, word : word + P], ident_f32[:])
            copy_out(
                nc,
                engine,
                x_grouped[:].bitcast(F32).rearrange("p (r u) -> p r u", u=2)[:, b * X_KEYS : (b + 1) * X_KEYS, :],
                bank[:].rearrange("p (u r) -> p r u", u=2),
            )

        def quantise_x(b):
            keys = slice(b * X_KEYS, (b + 1) * X_KEYS)
            nc.vector.quantize_mx(
                out=x_codes[:, keys].bitcast(FP8X4),
                scales=x_scales[:, keys],
                in_=x_grouped[:, keys.start * PACK : keys.stop * PACK],
            )

        def project_values(g, c, engine):
            bank = psum.tile([P, BANK], F32, name="bank")
            for j in range(PACK):
                keys = slice((PACK * g + j) * P, (PACK * g + j + 1) * P)
                nc.tensor.matmul_mx(
                    out=bank[:, j * P : (j + 1) * P],
                    lhsT=x_codes[:, keys].bitcast(FP8X4),
                    lhsT_scale=x_scales[:, keys],
                    rhs=w_codes[:, c * P : (c + 1) * P].bitcast(FP8X4),
                    rhs_scale=w_scales[:, c * P : (c + 1) * P],
                    start=True,
                    stop=True,
                )
            first = (g * DV + c * P) * PACK
            copy_out(
                nc,
                engine,
                v_grouped[:, first : first + P * PACK].rearrange("p (w j) -> p w j", j=PACK),
                bank[:].rearrange("p (j w) -> p w j", j=PACK),
            )

        def quantise_values(g):
            nc.vector.quantize_mx(
                out=v_codes[:, g * DV : (g + 1) * DV].bitcast(FP8X4),
                scales=v_scales[:, g * DV : (g + 1) * DV],
                in_=v_grouped[:, g * DV * PACK : (g + 1) * DV * PACK],
            )

        def multiply_qk(n, half):
            bank = psum_qk.tile([P, BANK], F32, name="bank")
            for h in range(2):
                nc.tensor.matmul(
                    out=bank[:],
                    lhsT=qT_pairs[:, queries_of(n), h],
                    rhs=kT_pairs[:, half * BANK : (half + 1) * BANK, h],
                    start=(h == 0),
                    stop=(h == 1),
                )
            qk[n, half] = bank

        def add_scores(n, half):
            t = logits[n][:, half * BANK : (half + 1) * BANK]
            nc.vector.scalar_tensor_tensor(
                out=t, in0=qk[n, half][:], scalar=NEGATED_SCALE, in1=t, op0=ALU.mult, op1=ALU.add
            )

        def row_minimum(n):
            shifts[n] = small.tile([P, 1], F32, name="shift")
            nc.vector.tensor_reduce(out=shifts[n][:], in_=logits[n][:], axis=AXIS.X, op=ALU.min)


        def exponentials(n, begin=0, end=KEY_PASSES):
            if begin == 0:
                e_rows[n] = work.tile([P, L], BF16, name="e_bf16")
                row_sums[n] = []
            row_sum = small.tile([P, 1], F32, name="row_sum%d" % begin)
            keys = slice(begin * BANK, end * BANK)
            nc.scalar.activation(
                out=e_rows[n][:, keys],
                in_=logits[n][:, keys],
                func=ACT.Exp,
                bias=shifts[n][:],
                scale=-1.0,
                accum_out=row_sum[:],
            )
            row_sums[n].append(row_sum)

        def transpose_e(n, begin=0, end=KEY_PASSES):
            e_words = e_rows[n][:].bitcast(F32)
            bank = psum.tile([P, BANK], F32, name="bank")
            for column, word in enumerate(range(2 * begin, 2 * end)):
                nc.tensor.transpose(
                    bank[:, column * P : (column + 1) * P], e_words[:, word * P : (word + 1) * P], ident_f32[:]
                )
            e_keys_first[n, begin] = bank

        def group_e(n, engine, begin=0, end=KEY_PASSES):
            if begin == 0:
                e_grouped[n] = work.tile([P, L], BF16, name="e_grouped", align_bytes=64)
            copy_out(
                nc,
                engine,
                e_grouped[n][:].bitcast(F32).rearrange("p (g w u) -> p g w u", g=KEY_PASSES, u=2)[:, begin:end],
                e_keys_first[n, begin][:, : (end - begin) * 2 * P].rearrange("p (g u w) -> p g w u", u=2, w=P),
            )

        def quantise_e(n, begin=0, end=KEY_PASSES):
            if begin == 0:
                e_codes = work.tile([P, KEY_PASSES * P], U32, name="e_codes", align_bytes=64)
                e_scales = work.tile([P, KEY_PASSES * P], U8, name="e_scales", align_bytes=64)
                e_quantised[n] = (e_codes, e_scales)
            e_codes, e_scales = e_quantised[n]
            words = slice(begin * P, end * P)
            nc.vector.quantize_mx(
                out=e_codes[:, words].bitcast(FP8X4),
                scales=e_scales[:, words],
                in_=e_grouped[n][:, begin * BANK : end * BANK],
            )

        def total_row_sum(n):
            total = small.tile([P, 1], F32, name="total")
            nc.vector.tensor_tensor(out=total[:], in0=row_sums[n][0][:], in1=row_sums[n][1][:], op=ALU.add)
            row_sums[n] = [total]

        def invert_row_sum(n):
            inverses[n] = small.tile([P, 1], F32, name="inverse")
            nc.vector.reciprocal(out=inverses[n][:], in_=row_sums[n][0][:])

        def multiply_e_v(n, parts=1):
            e_codes, e_scales = e_quantised[n]
            width = DV // parts
            sums[n] = []
            for part in range(parts):
                bank = psum.tile([P, BANK], F32, name="bank")
                for g in range(KEY_PASSES):
                    cols = slice(g * DV + part * width, g * DV + (part + 1) * width)
                    nc.tensor.matmul_mx(
                        out=bank[:, :width],
                        lhsT=e_codes[:, g * P : (g + 1) * P].bitcast(FP8X4),
                        lhsT_scale=e_scales[:, g * P : (g + 1) * P],
                        rhs=v_codes[:, cols].bitcast(FP8X4),
                        rhs_scale=v_scales[:, cols],
                        start=(g == 0),
                        stop=(g == KEY_PASSES - 1),
                    )
                sums[n].append(bank)

        def normalise(n, *engines):
            normalised[n] = results.tile([P, DV], F32, name="result")
            width = DV // len(engines)
            for part, engine in enumerate(engines):
                cols = slice(part * width, (part + 1) * width)
                scaled_copy_out(nc, engine, normalised[n][:, cols], sums[n][part][:, :width], inverses[n][:])

        def store_result(n):
            nc.sync.dma_start(out=out_rows[queries_of(n), :], in_=normalised[n][:])

        turns = (VECTOR, SCALAR, VECTOR, SCALAR)
        keep_clock(4)
        transpose_chunk("q", 768, SCALAR)
        keep_clock(1)
        for index, engine in enumerate(turns):
            transpose_chunk("e", 2 * P * index, engine)
        group_w()
        compute_z(0, (VECTOR, SCALAR))
        store_z(0)
        transpose_chunk("q", 512, VECTOR)
        compute_z(1, (VECTOR, SCALAR))
        store_z(1)
        load_chunk("q", q_rows, 0, 4)
        transpose_x(0, VECTOR)
        transpose_x(1, SCALAR)
        transpose_chunk("k", 0, SCALAR)
        quantise_w()
        quantise_x(0)
        quantise_x(1)
        compute_z(2, (VECTOR, SCALAR))
        read_windows(0)
        store_z(2)
        read_windows(1)
        for c, engine in enumerate(turns):
            project_values(0, c, engine)
        transpose_x(2, VECTOR)
        transpose_x(3, SCALAR)
        transpose_chunk("k", 512, SCALAR)
        quantise_x(2)
        quantise_x(3)
        compute_z(3, (VECTOR, SCALAR))
        store_z(3)
        read_windows(2)
        transpose_chunk("q", 0, SCALAR)
        multiply_qk(0, 0)
        project_values(1, 0, VECTOR)
        multiply_qk(0, 1)
        project_values(1, 1, SCALAR)
        project_values(1, 2, SCALAR)

        for n in range(STEPS):
            if n >= 1:
                exponentials(n - 1)
            add_scores(n, 0)
            add_scores(n, 1)
            if n + Z_AHEAD < STEPS:
                compute_z(n + Z_AHEAD, (SCALAR, SCALAR))
                store_z(n + Z_AHEAD)
            if n == 0:
                project_values(1, 3, SCALAR)
            if n >= 2:
                group_e(n - 2, SCALAR)
            if n >= E_LAG + 1:
                normalise(n - E_LAG - 1, SCALAR)
            if n < KEY_PASSES:
                quantise_values(n)
            if n >= E_LAG:
                invert_row_sum(n - E_LAG)
                quantise_e(n - E_LAG)
            row_minimum(n)
            if n + 1 < STEPS:
                multiply_qk(n + 1, 0)
                multiply_qk(n + 1, 1)
            if n + Z_AHEAD - 1 < STEPS:
                read_windows(n + Z_AHEAD - 1)
            if n >= E_LAG + 1:
                store_result(n - E_LAG - 1)
            if n >= 1:
                transpose_e(n - 1)
            if n >= E_LAG:
                multiply_e_v(n - E_LAG)
            if n >= STEPS - 2:
                keep_clock(2)

        last = STEPS - 1
        for g in range(KEY_PASSES):
            exponentials(last, g, g + 1)
        invert_row_sum(last - 2)
        quantise_e(last - 2)
        multiply_e_v(last - 2)
        group_e(last - 1, VECTOR)
        invert_row_sum(last - 1)
        transpose_e(last, 0, 1)
        quantise_e(last - 1)
        group_e(last, VECTOR, 0, 1)
        transpose_e(last, 1, 2)
        total_row_sum(last)
        group_e(last, VECTOR, 1, 2)
        quantise_e(last, 0, 1)
        invert_row_sum(last)
        quantise_e(last, 1, 2)
        normalise(last - 3, SCALAR)
        store_result(last - 3)
        multiply_e_v(last - 1)
        normalise(last - 2, SCALAR)
        store_result(last - 2)
        multiply_e_v(last, 2)
        normalise(last - 1, VECTOR)
        store_result(last - 1)
        normalise(last, SCALAR, VECTOR)
        store_result(last)
